import numpy as np
import ml_dtypes


def mxq(x, axis, fmt="e4m3"):
    dtype, down = {"e4m3": (ml_dtypes.float8_e4m3fn, 7), "e5m2": (ml_dtypes.float8_e5m2, 14)}[fmt]
    v = np.moveaxis(np.asarray(x, np.float32).astype(ml_dtypes.bfloat16).astype(np.float64), axis, -1)
    blocks = v.reshape(v.shape[:-1] + (-1, 32))
    amax = np.abs(blocks).max(-1, keepdims=True)
    byte = np.maximum(np.where(amax > 0, np.frexp(amax)[1] - 1 + 127, 0) - down, 1)
    scale = np.exp2(byte - 127.0)
    codes = (blocks / scale).astype(np.float32).astype(dtype).astype(np.float64)
    return np.moveaxis((codes * scale).reshape(v.shape), -1, axis)


WIDE = False


def mx_kscale(k):
    if not WIDE:
        return np.ones(k)
    levels = np.array([10, -10, 5, -5, 0])
    a = np.random.permutation(np.resize(levels, k // 512 * 4)).reshape(k // 512, 4)
    idx = np.arange(k)
    return np.exp2(a[idx // 512, idx % 128 // 32])


BF16 = ml_dtypes.bfloat16


def bf(x):
    return np.asarray(x, np.float32).astype(BF16)


def f64(x):
    return np.asarray(x).astype(np.float64)


B, C_IN, C_OUT, K_SIZE, STRIDE, PAD, H = 2, 256, 128, 2, 1, 1, 31
H_OUT = (H + 2 * PAD - K_SIZE) // STRIDE + 1
KK = C_IN * K_SIZE * K_SIZE
BLK = 32
RUN = int(np.lcm(BLK, K_SIZE * K_SIZE)) // (K_SIZE * K_SIZE)


def setup_inputs():
    s = mx_kscale(KK)
    sc = s[(np.arange(C_IN) // RUN) * RUN * K_SIZE * K_SIZE]
    sf = np.repeat(sc, K_SIZE * K_SIZE)
    x = np.random.standard_normal((B, C_IN, H, H)) * sc[None, :, None, None]
    Kf = np.random.uniform(-1.0, 1.0, (KK, C_OUT)) * np.sqrt(3.0 / KK) / sf[:, None]
    return {"x": bf(x), "K": bf(Kf.reshape(K_SIZE, K_SIZE, C_IN, C_OUT))}


def reference(x, K):
    xp = np.pad(f64(x), ((0, 0), (0, 0), (PAD, PAD), (PAD, PAD)))
    end = (H_OUT - 1) * STRIDE + 1
    rows = []
    for di in range(K_SIZE):
        cols = []
        for dj in range(K_SIZE):
            cols.append(xp[:, :, di:di + end:STRIDE, dj:dj + end:STRIDE])
        rows.append(np.stack(cols, axis=2))
    patches = np.stack(rows, axis=2)
    p = patches.transpose(0, 4, 5, 1, 2, 3).reshape(B, H_OUT, H_OUT, -1)
    Kf = f64(K).reshape(-1, C_OUT)
    out = mxq(p, 3, "e4m3") @ mxq(Kf, 0, "e4m3")
    return out.transpose(0, 3, 1, 2)

@@ -1,0 +1,131 @@
+from contextlib import ExitStack
+
+import concourse.mybir as mybir
+
+BF16 = mybir.dt.bfloat16
+F32 = mybir.dt.float32
+U32 = mybir.dt.uint32
+U8 = mybir.dt.uint8
+FP8X4 = mybir.dt.float8_e4m3fn_x4
+
+P = 128
+PACK = 4
+BATCH = 2
+C_IN = 256
+C_OUT = 128
+H = 31
+H_OUT = 32
+IMG = H * H
+PASSES = C_IN // P
+HALF = H_OUT // 2
+CLASS_COLS = HALF * HALF
+
+BLOCK = 16
+LEAD = H + 1
+COPY_LEN = -(-(LEAD + 1 + IMG + H + 1) // BLOCK) * BLOCK
+COPY_WORDS = COPY_LEN // 2
+HEAD_END = -(-(LEAD + 1) // BLOCK) * BLOCK
+TAIL_START = (LEAD + IMG) // BLOCK * BLOCK
+
+FLOPS = 2 * BATCH * H_OUT * H_OUT * C_IN * PACK * C_OUT
+
+
+def word_of_pair(ip, jp, di):
+    element = LEAD + H * (ip + di - 1) + (jp - 1)
+    odd = element % 2
+    return odd * COPY_WORDS + (element + odd) // 2
+
+
+def tile_conv2d_s_kernel(tc, x, K, out):
+    nc = tc.nc
+    with ExitStack() as ctx:
+        keep = ctx.enter_context(tc.tile_pool(name="keep", bufs=1))
+        banks = ctx.enter_context(tc.psum_pool(name="banks", bufs=1))
+
+        k_rows = keep.tile([P, PASSES, PACK, C_OUT], BF16, name="k_rows")
+        nc.sync.dma_start(
+            out=k_rows[:].rearrange("q g t o -> q g (t o)"),
+            in_=K.rearrange("kh kw c o -> (kh kw c) o").rearrange("(g q t) o -> q g (t o)", g=PASSES, q=P),
+        )
+
+        images = {}
+        for b in range(BATCH):
+            for g in range(PASSES):
+                image = keep.tile([P, 3 * COPY_LEN], BF16, name="image_%d_%d" % (b, g))
+                images[(b, g)] = image
+                both = image[:, 0 : 2 * COPY_LEN].rearrange("q (v l) -> q v l", v=2)
+                nc.vector.memset(both[:, :, 0:HEAD_END], 0.0)
+                nc.vector.memset(both[:, :, TAIL_START:COPY_LEN], 0.0)
+                channels = x[b, g * P : (g + 1) * P].rearrange("c h w -> c (h w)")
+                nc.sync.dma_start(out=image[:, LEAD : LEAD + IMG], in_=channels)
+                nc.sync.dma_start(out=image[:, COPY_LEN + LEAD + 1 : COPY_LEN + LEAD + 1 + IMG], in_=channels)
+
+        k_grouped = keep.tile([P, PASSES, 2, C_OUT, PACK], BF16, name="k_grouped", align_bytes=64)
+        nc.vector.tensor_copy(out=k_grouped[:, :, 0, :, :], in_=k_rows[:].rearrange("q g t o -> q g o t"))
+        for first in range(2):
+            nc.vector.tensor_copy(
+                out=k_grouped[:, :, 1, :, 2 * first : 2 * first + 2],
+                in_=k_rows[:, :, 2 * (1 - first) : 2 * (1 - first) + 2, :].rearrange("q g t o -> q g o t"),
+            )
+        k_codes = keep.tile([P, PASSES, 2, C_OUT], U32, name="k_codes", align_bytes=64)
+        k_scales = keep.tile([P, PASSES, 2, C_OUT], U8, name="k_scales", align_bytes=64)
+        nc.vector.quantize_mx(
+            out=k_codes[:].rearrange("q g v o -> q (g v o)").bitcast(FP8X4),
+            scales=k_scales[:].rearrange("q g v o -> q (g v o)"),
+            in_=k_grouped[:].rearrange("q g v o t -> q (g v o t)"),
+        )
+
+        def windows_of_class(image, ip, jp):
+            words = [word_of_pair(ip, jp, di) for di in range(2)]
+            start = min(words)
+            step = max(words) - start
+            two_rows = image[:].bitcast(F32)[:, start : start + 2 * step].rearrange("q (d f) -> q d f", d=2)
+            grid = two_rows[:, :, 0 : HALF * H].rearrange("q d (a r) -> q d a r", r=H)[:, :, :, 0:HALF]
+            return grid.rearrange("q d a m -> q a m d")
+
+        for b in range(BATCH):
+            p_codes = {}
+            p_scales = {}
+            for g in range(PASSES):
+                for ip in range(2):
+                    windows = keep.tile(
+                        [P, 2 * CLASS_COLS * PACK], BF16, name="windows_%d_%d_%d" % (b, g, ip), align_bytes=64
+                    )
+                    pairs = windows[:].bitcast(F32).rearrange("q (jp a m d) -> q jp a m d", jp=2, a=HALF, m=HALF)
+                    nc.vector.tensor_copy(out=pairs[:, 0], in_=windows_of_class(images[(b, g)], ip, 0))
+                    nc.scalar.copy(out=pairs[:, 1], in_=windows_of_class(images[(b, g)], ip, 1))
+                    values = windows[:].rearrange(
+                        "q (jp a m d dj) -> q jp a m d dj", jp=2, a=HALF, m=HALF, d=2
+                    )
+                    nc.vector.memset(values[:, 0, :, 0, :, 0], 0.0)
+                    nc.vector.memset(values[:, 1, :, HALF - 1, :, 1], 0.0)
+
+                    codes = keep.tile([P, 2 * CLASS_COLS], U32, name="codes_%d_%d_%d" % (b, g, ip), align_bytes=64)
+                    scales = keep.tile([P, 2 * CLASS_COLS], U8, name="scales_%d_%d_%d" % (b, g, ip), align_bytes=64)
+                    nc.vector.quantize_mx(out=codes[:].bitcast(FP8X4), scales=scales[:], in_=windows[:])
+                    p_codes[(g, ip)] = codes
+                    p_scales[(g, ip)] = scales
+
+            result = keep.tile([P, H_OUT * H_OUT], F32, name="result_%d" % b)
+            rows = result[:].rearrange("o (a ip m jp) -> o ip a m jp", a=HALF, ip=2, m=HALF)
+            for ip in range(2):
+                acc = banks.tile([P, 2 * CLASS_COLS], F32, name="acc_%d_%d" % (b, ip))
+                for jp in range(2):
+                    cols = slice(jp * CLASS_COLS, (jp + 1) * CLASS_COLS)
+                    flipped = 0 if word_of_pair(ip, jp, 0) < word_of_pair(ip, jp, 1) else 1
+                    for g in range(PASSES):
+                        nc.tensor.matmul_mx(
+                            out=acc[:, cols],
+                            lhsT=k_codes[:, g, flipped, :].bitcast(FP8X4),
+                            lhsT_scale=k_scales[:, g, flipped, :],
+                            rhs=p_codes[(g, ip)][:, cols].bitcast(FP8X4),
+                            rhs_scale=p_scales[(g, ip)][:, cols],
+                            start=(g == 0),
+                            stop=(g == PASSES - 1),
+                        )
+                in_order = acc[:].rearrange("o (jp a m) -> o a m jp", jp=2, a=HALF)
+                if ip == 0:
+                    nc.vector.tensor_copy(out=rows[:, ip], in_=in_order)
+                else:
+                    nc.scalar.copy(out=rows[:, ip], in_=in_order)
+            nc.sync.dma_start(out=out[b].rearrange("o i j -> o (i j)"), in_=result[:])

@@ -38,9 +38,11 @@ def word_of_pair(ip, jp, di):
 
 def tile_conv2d_s_kernel(tc, x, K, out):
     nc = tc.nc
+    chunks = [(b, g) for b in range(BATCH) for g in range(PASSES)]
     with ExitStack() as ctx:
         keep = ctx.enter_context(tc.tile_pool(name="keep", bufs=1))
         banks = ctx.enter_context(tc.psum_pool(name="banks", bufs=1))
+        ctx.enter_context(tc.manual_schedule())
 
         k_rows = keep.tile([P, PASSES, PACK, C_OUT], BF16, name="k_rows")
         nc.sync.dma_start(
@@ -49,31 +51,29 @@ def tile_conv2d_s_kernel(tc, x, K, out):
         )
 
         images = {}
-        for b in range(BATCH):
-            for g in range(PASSES):
-                image = keep.tile([P, 3 * COPY_LEN], BF16, name="image_%d_%d" % (b, g))
-                images[(b, g)] = image
-                both = image[:, 0 : 2 * COPY_LEN].rearrange("q (v l) -> q v l", v=2)
-                nc.vector.memset(both[:, :, 0:HEAD_END], 0.0)
-                nc.vector.memset(both[:, :, TAIL_START:COPY_LEN], 0.0)
-                channels = x[b, g * P : (g + 1) * P].rearrange("c h w -> c (h w)")
-                nc.sync.dma_start(out=image[:, LEAD : LEAD + IMG], in_=channels)
-                nc.sync.dma_start(out=image[:, COPY_LEN + LEAD + 1 : COPY_LEN + LEAD + 1 + IMG], in_=channels)
+        for b, g in chunks:
+            image = keep.tile([P, 3 * COPY_LEN], BF16, name="image_%d_%d" % (b, g))
+            images[(b, g)] = image
+            both = image[:, 0 : 2 * COPY_LEN].rearrange("q (v l) -> q v l", v=2)
+            nc.vector.memset(both[:, :, 0:HEAD_END], 0.0)
+            nc.vector.memset(both[:, :, TAIL_START:COPY_LEN], 0.0)
+            channels = x[b, g * P : (g + 1) * P].rearrange("c h w -> c (h w)")
+            twice = image[:, LEAD : LEAD + 2 * (COPY_LEN + 1)].rearrange("q (v l) -> q v l", v=2)
+            nc.sync.dma_start(out=twice[:, :, 0:IMG], in_=channels.unsqueeze(1).to_broadcast([P, 2, IMG]))
 
-        k_grouped = keep.tile([P, PASSES, 2, C_OUT, PACK], BF16, name="k_grouped", align_bytes=64)
-        nc.vector.tensor_copy(out=k_grouped[:, :, 0, :, :], in_=k_rows[:].rearrange("q g t o -> q g o t"))
-        for first in range(2):
-            nc.vector.tensor_copy(
-                out=k_grouped[:, :, 1, :, 2 * first : 2 * first + 2],
-                in_=k_rows[:, :, 2 * (1 - first) : 2 * (1 - first) + 2, :].rearrange("q g t o -> q g o t"),
+        zeros = keep.tile([P, 2 * HALF * 2], BF16, name="zeros")
+        nc.vector.memset(zeros[:], 0.0)
+
+        k_grouped = keep.tile([P, 2, PASSES, C_OUT, PACK], BF16, name="k_grouped", align_bytes=64)
+        k_codes = keep.tile([P, 2, PASSES, C_OUT], U32, name="k_codes", align_bytes=64)
+        k_scales = keep.tile([P, 2, PASSES, C_OUT], U8, name="k_scales", align_bytes=64)
+
+        def quantise_k(flipped):
+            nc.vector.quantize_mx(
+                out=k_codes[:, flipped].rearrange("q g o -> q (g o)").bitcast(FP8X4),
+                scales=k_scales[:, flipped].rearrange("q g o -> q (g o)"),
+                in_=k_grouped[:, flipped].rearrange("q g o t -> q (g o t)"),
             )
-        k_codes = keep.tile([P, PASSES, 2, C_OUT], U32, name="k_codes", align_bytes=64)
-        k_scales = keep.tile([P, PASSES, 2, C_OUT], U8, name="k_scales", align_bytes=64)
-        nc.vector.quantize_mx(
-            out=k_codes[:].rearrange("q g v o -> q (g v o)").bitcast(FP8X4),
-            scales=k_scales[:].rearrange("q g v o -> q (g v o)"),
-            in_=k_grouped[:].rearrange("q g v o t -> q (g v o t)"),
-        )
 
         def windows_of_class(image, ip, jp):
             words = [word_of_pair(ip, jp, di) for di in range(2)]
@@ -83,29 +83,50 @@ def tile_conv2d_s_kernel(tc, x, K, out):
             grid = two_rows[:, :, 0 : HALF * H].rearrange("q d (a r) -> q d a r", r=H)[:, :, :, 0:HALF]
             return grid.rearrange("q d a m -> q a m d")
 
+        windows = {}
+        p_codes = {}
+        p_scales = {}
+
+        def build_windows(chunk):
+            tile = keep.tile([P, 2, 2 * CLASS_COLS * PACK], BF16, name="windows_%d_%d" % chunk, align_bytes=64)
+            windows[chunk] = tile
+            pairs = tile[:].bitcast(F32).rearrange("q ip (jp a m d) -> q ip jp a m d", jp=2, a=HALF, m=HALF)
+            values = tile[:].rearrange("q ip (jp a m d dj) -> q ip jp a m d dj", jp=2, a=HALF, m=HALF, d=2)
+            for ip in range(2):
+                nc.vector.tensor_copy(out=pairs[:, ip, 0], in_=windows_of_class(images[chunk], ip, 0))
+                nc.scalar.copy(out=pairs[:, ip, 1], in_=windows_of_class(images[chunk], ip, 1))
+            padding = zeros[:].rearrange("q (ip a d) -> q ip a d", ip=2, a=HALF)
+            nc.scalar.copy(out=values[:, :, 0, :, 0, :, 0], in_=padding)
+            nc.scalar.copy(out=values[:, :, 1, :, HALF - 1, :, 1], in_=padding)
+
+        def quantise_windows(chunk):
+            codes = keep.tile([P, 2, 2, CLASS_COLS], U32, name="codes_%d_%d" % chunk, align_bytes=64)
+            scales = keep.tile([P, 2, 2, CLASS_COLS], U8, name="scales_%d_%d" % chunk, align_bytes=64)
+            by_class = windows[chunk][:].rearrange("q ip (jp n) -> q ip jp n", jp=2)
+            for ip in range(2):
+                for jp in range(2):
+                    nc.vector.quantize_mx(
+                        out=codes[:, ip, jp].bitcast(FP8X4), scales=scales[:, ip, jp], in_=by_class[:, ip, jp]
+                    )
+            p_codes[chunk] = codes
+            p_scales[chunk] = scales
+
+        nc.vector.tensor_copy(out=k_grouped[:, 0], in_=k_rows[:].rearrange("q g t o -> q g o t"))
+        for di in range(2):
+            nc.scalar.copy(
+                out=k_grouped[:, 1, :, :, 2 * (1 - di) : 2 * (1 - di) + 2],
+                in_=k_rows[:, :, 2 * di : 2 * di + 2, :].rearrange("q g t o -> q g o t"),
+            )
+        quantise_k(0)
+
+        build_windows(chunks[0])
+        quantise_k(1)
+        for n in range(1, len(chunks)):
+            build_windows(chunks[n])
+            quantise_windows(chunks[n - 1])
+        quantise_windows(chunks[-1])
+
         for b in range(BATCH):
-            p_codes = {}
-            p_scales = {}
-            for g in range(PASSES):
-                for ip in range(2):
-                    windows = keep.tile(
-                        [P, 2 * CLASS_COLS * PACK], BF16, name="windows_%d_%d_%d" % (b, g, ip), align_bytes=64
-                    )
-                    pairs = windows[:].bitcast(F32).rearrange("q (jp a m d) -> q jp a m d", jp=2, a=HALF, m=HALF)
-                    nc.vector.tensor_copy(out=pairs[:, 0], in_=windows_of_class(images[(b, g)], ip, 0))
-                    nc.scalar.copy(out=pairs[:, 1], in_=windows_of_class(images[(b, g)], ip, 1))
-                    values = windows[:].rearrange(
-                        "q (jp a m d dj) -> q jp a m d dj", jp=2, a=HALF, m=HALF, d=2
-                    )
-                    nc.vector.memset(values[:, 0, :, 0, :, 0], 0.0)
-                    nc.vector.memset(values[:, 1, :, HALF - 1, :, 1], 0.0)
-
-                    codes = keep.tile([P, 2 * CLASS_COLS], U32, name="codes_%d_%d_%d" % (b, g, ip), align_bytes=64)
-                    scales = keep.tile([P, 2 * CLASS_COLS], U8, name="scales_%d_%d_%d" % (b, g, ip), align_bytes=64)
-                    nc.vector.quantize_mx(out=codes[:].bitcast(FP8X4), scales=scales[:], in_=windows[:])
-                    p_codes[(g, ip)] = codes
-                    p_scales[(g, ip)] = scales
-
             result = keep.tile([P, H_OUT * H_OUT], F32, name="result_%d" % b)
             rows = result[:].rearrange("o (a ip m jp) -> o ip a m jp", a=HALF, ip=2, m=HALF)
             for ip in range(2):
@@ -116,16 +137,17 @@ def tile_conv2d_s_kernel(tc, x, K, out):
                     for g in range(PASSES):
                         nc.tensor.matmul_mx(
                             out=acc[:, cols],
-                            lhsT=k_codes[:, g, flipped, :].bitcast(FP8X4),
-                            lhsT_scale=k_scales[:, g, flipped, :],
-                            rhs=p_codes[(g, ip)][:, cols].bitcast(FP8X4),
-                            rhs_scale=p_scales[(g, ip)][:, cols],
+                            lhsT=k_codes[:, flipped, g, :].bitcast(FP8X4),
+                            lhsT_scale=k_scales[:, flipped, g, :],
+                            rhs=p_codes[(b, g)][:, ip, jp].bitcast(FP8X4),
+                            rhs_scale=p_scales[(b, g)][:, ip, jp],
                             start=(g == 0),
                             stop=(g == PASSES - 1),
                         )
                 in_order = acc[:].rearrange("o (jp a m) -> o a m jp", jp=2, a=HALF)
-                if ip == 0:
-                    nc.vector.tensor_copy(out=rows[:, ip], in_=in_order)
-                else:
-                    nc.scalar.copy(out=rows[:, ip], in_=in_order)
-            nc.sync.dma_start(out=out[b].rearrange("o i j -> o (i j)"), in_=result[:])
+                for part in range(2):
+                    some = slice(part * (HALF // 2), (part + 1) * (HALF // 2))
+                    nc.scalar.copy(out=rows[:, ip, some], in_=in_order[:, some])
+            for part in range(2):
+                some = slice(part * (H_OUT * HALF), (part + 1) * (H_OUT * HALF))
+                nc.sync.dma_start(out=out[b].rearrange("o i j -> o (i j)")[:, some], in_=result[:, some])

@@ -18,7 +18,9 @@ H_OUT = 32
 IMG = H * H
 PASSES = C_IN // P
 HALF = H_OUT // 2
-CLASS_COLS = HALF * HALF
+PARTS = 2
+PART_ROWS = HALF // PARTS
+GROUP_COLS = 2 * PART_ROWS * HALF
 
 BLOCK = 16
 LEAD = H + 1
@@ -61,66 +63,63 @@ def tile_conv2d_s_kernel(tc, x, K, out):
             twice = image[:, LEAD : LEAD + 2 * (COPY_LEN + 1)].rearrange("q (v l) -> q v l", v=2)
             nc.sync.dma_start(out=twice[:, :, 0:IMG], in_=channels.unsqueeze(1).to_broadcast([P, 2, IMG]))
 
-        zeros = keep.tile([P, 2 * HALF * 2], BF16, name="zeros")
+        zeros = keep.tile([P, H_OUT * 2], BF16, name="zeros")
         nc.vector.memset(zeros[:], 0.0)
 
-        k_grouped = keep.tile([P, 2, PASSES, C_OUT, PACK], BF16, name="k_grouped", align_bytes=64)
-        k_codes = keep.tile([P, 2, PASSES, C_OUT], U32, name="k_codes", align_bytes=64)
-        k_scales = keep.tile([P, 2, PASSES, C_OUT], U8, name="k_scales", align_bytes=64)
-
-        def quantise_k(flipped):
-            nc.vector.quantize_mx(
-                out=k_codes[:, flipped].rearrange("q g o -> q (g o)").bitcast(FP8X4),
-                scales=k_scales[:, flipped].rearrange("q g o -> q (g o)"),
-                in_=k_grouped[:, flipped].rearrange("q g o t -> q (g o t)"),
-            )
+        k_grouped = keep.tile([P, PASSES, C_OUT, PACK], BF16, name="k_grouped", align_bytes=64)
+        k_codes = keep.tile([P, PASSES, C_OUT], U32, name="k_codes", align_bytes=64)
+        k_scales = keep.tile([P, PASSES, C_OUT], U8, name="k_scales", align_bytes=64)
+        side_by_side = k_rows[:].rearrange("q g t o -> q g o t")
+        nc.vector.tensor_copy(out=k_grouped[:, 0], in_=side_by_side[:, 0])
+        nc.scalar.copy(out=k_grouped[:, 1], in_=side_by_side[:, 1])
+        nc.vector.quantize_mx(
+            out=k_codes[:].rearrange("q g o -> q (g o)").bitcast(FP8X4),
+            scales=k_scales[:].rearrange("q g o -> q (g o)"),
+            in_=k_grouped[:].rearrange("q g o t -> q (g o t)"),
+        )
 
         def windows_of_class(image, ip, jp):
             words = [word_of_pair(ip, jp, di) for di in range(2)]
             start = min(words)
-            step = max(words) - start
-            two_rows = image[:].bitcast(F32)[:, start : start + 2 * step].rearrange("q (d f) -> q d f", d=2)
+            apart = max(words) - start
+            two_rows = image[:].bitcast(F32)[:, start : start + 2 * apart].rearrange("q (d f) -> q d f", d=2)
+            if words[0] > words[1]:
+                two_rows = two_rows[:, ::-1]
             grid = two_rows[:, :, 0 : HALF * H].rearrange("q d (a r) -> q d a r", r=H)[:, :, :, 0:HALF]
-            return grid.rearrange("q d a m -> q a m d")
+            return grid.rearrange("q d (part a) m -> q part a m d", part=PARTS)
 
         windows = {}
         p_codes = {}
         p_scales = {}
 
         def build_windows(chunk):
-            tile = keep.tile([P, 2, 2 * CLASS_COLS * PACK], BF16, name="windows_%d_%d" % chunk, align_bytes=64)
+            tile = keep.tile([P, 2, PARTS, GROUP_COLS * PACK], BF16, name="windows_%d_%d" % chunk, align_bytes=64)
             windows[chunk] = tile
-            pairs = tile[:].bitcast(F32).rearrange("q ip (jp a m d) -> q ip jp a m d", jp=2, a=HALF, m=HALF)
-            values = tile[:].rearrange("q ip (jp a m d dj) -> q ip jp a m d dj", jp=2, a=HALF, m=HALF, d=2)
+            pairs = tile[:].bitcast(F32).rearrange("q ip part (jp a m d) -> q ip jp part a m d", jp=2, a=PART_ROWS, m=HALF)
+            values = tile[:].rearrange(
+                "q ip part (jp a m d dj) -> q jp m dj (ip part) a d", jp=2, a=PART_ROWS, m=HALF, d=2
+            )
             for ip in range(2):
                 nc.vector.tensor_copy(out=pairs[:, ip, 0], in_=windows_of_class(images[chunk], ip, 0))
                 nc.scalar.copy(out=pairs[:, ip, 1], in_=windows_of_class(images[chunk], ip, 1))
-            padding = zeros[:].rearrange("q (ip a d) -> q ip a d", ip=2, a=HALF)
-            nc.scalar.copy(out=values[:, :, 0, :, 0, :, 0], in_=padding)
-            nc.scalar.copy(out=values[:, :, 1, :, HALF - 1, :, 1], in_=padding)
+            padding = zeros[:].rearrange("q (n a d) -> q n a d", a=PART_ROWS, d=2)
+            nc.scalar.copy(out=values[:, 0, 0, 0], in_=padding)
+            nc.scalar.copy(out=values[:, 1, HALF - 1, 1], in_=padding)
 
         def quantise_windows(chunk):
-            codes = keep.tile([P, 2, 2, CLASS_COLS], U32, name="codes_%d_%d" % chunk, align_bytes=64)
-            scales = keep.tile([P, 2, 2, CLASS_COLS], U8, name="scales_%d_%d" % chunk, align_bytes=64)
-            by_class = windows[chunk][:].rearrange("q ip (jp n) -> q ip jp n", jp=2)
+            codes = keep.tile([P, 2, PARTS, GROUP_COLS], U32, name="codes_%d_%d" % chunk, align_bytes=64)
+            scales = keep.tile([P, 2, PARTS, GROUP_COLS], U8, name="scales_%d_%d" % chunk, align_bytes=64)
             for ip in range(2):
-                for jp in range(2):
+                for part in range(PARTS):
                     nc.vector.quantize_mx(
-                        out=codes[:, ip, jp].bitcast(FP8X4), scales=scales[:, ip, jp], in_=by_class[:, ip, jp]
+                        out=codes[:, ip, part].bitcast(FP8X4),
+                        scales=scales[:, ip, part],
+                        in_=windows[chunk][:, ip, part],
                     )
             p_codes[chunk] = codes
             p_scales[chunk] = scales
 
-        nc.vector.tensor_copy(out=k_grouped[:, 0], in_=k_rows[:].rearrange("q g t o -> q g o t"))
-        for di in range(2):
-            nc.scalar.copy(
-                out=k_grouped[:, 1, :, :, 2 * (1 - di) : 2 * (1 - di) + 2],
-                in_=k_rows[:, :, 2 * di : 2 * di + 2, :].rearrange("q g t o -> q g o t"),
-            )
-        quantise_k(0)
-
         build_windows(chunks[0])
-        quantise_k(1)
         for n in range(1, len(chunks)):
             build_windows(chunks[n])
             quantise_windows(chunks[n - 1])
@@ -128,26 +127,23 @@ def tile_conv2d_s_kernel(tc, x, K, out):
 
         for b in range(BATCH):
             result = keep.tile([P, H_OUT * H_OUT], F32, name="result_%d" % b)
-            rows = result[:].rearrange("o (a ip m jp) -> o ip a m jp", a=HALF, ip=2, m=HALF)
+            rows = result[:].rearrange("o (part a ip m jp) -> o ip part a m jp", part=PARTS, a=PART_ROWS, ip=2, m=HALF)
             for ip in range(2):
-                acc = banks.tile([P, 2 * CLASS_COLS], F32, name="acc_%d_%d" % (b, ip))
-                for jp in range(2):
-                    cols = slice(jp * CLASS_COLS, (jp + 1) * CLASS_COLS)
-                    flipped = 0 if word_of_pair(ip, jp, 0) < word_of_pair(ip, jp, 1) else 1
+                for part in range(PARTS):
+                    acc = banks.tile([P, GROUP_COLS], F32, name="acc_%d_%d_%d" % (b, ip, part))
                     for g in range(PASSES):
                         nc.tensor.matmul_mx(
-                            out=acc[:, cols],
-                            lhsT=k_codes[:, flipped, g, :].bitcast(FP8X4),
-                            lhsT_scale=k_scales[:, flipped, g, :],
-                            rhs=p_codes[(b, g)][:, ip, jp].bitcast(FP8X4),
-                            rhs_scale=p_scales[(b, g)][:, ip, jp],
+                            out=acc[:],
+                            lhsT=k_codes[:, g].bitcast(FP8X4),
+                            lhsT_scale=k_scales[:, g],
+                            rhs=p_codes[(b, g)][:, ip, part].bitcast(FP8X4),
+                            rhs_scale=p_scales[(b, g)][:, ip, part],
                             start=(g == 0),
                             stop=(g == PASSES - 1),
                         )
-                in_order = acc[:].rearrange("o (jp a m) -> o a m jp", jp=2, a=HALF)
-                for part in range(2):
-                    some = slice(part * (HALF // 2), (part + 1) * (HALF // 2))
-                    nc.scalar.copy(out=rows[:, ip, some], in_=in_order[:, some])
-            for part in range(2):
+                    nc.scalar.copy(
+                        out=rows[:, ip, part], in_=acc[:].rearrange("o (jp a m) -> o a m jp", jp=2, a=PART_ROWS)
+                    )
+            for part in range(PARTS):
                 some = slice(part * (H_OUT * HALF), (part + 1) * (H_OUT * HALF))
                 nc.sync.dma_start(out=out[b].rearrange("o i j -> o (i j)")[:, some], in_=result[:, some])

@@ -60,8 +60,10 @@ def tile_conv2d_s_kernel(tc, x, K, out):
             nc.vector.memset(both[:, :, 0:HEAD_END], 0.0)
             nc.vector.memset(both[:, :, TAIL_START:COPY_LEN], 0.0)
             channels = x[b, g * P : (g + 1) * P].rearrange("c h w -> c (h w)")
-            twice = image[:, LEAD : LEAD + 2 * (COPY_LEN + 1)].rearrange("q (v l) -> q v l", v=2)
-            nc.sync.dma_start(out=twice[:, :, 0:IMG], in_=channels.unsqueeze(1).to_broadcast([P, 2, IMG]))
+            odd_start = COPY_LEN + LEAD + 1
+            nc.sync.dma_start(out=image[:, LEAD : LEAD + IMG], in_=channels)
+            nc.sync.dma_start(out=image[:, odd_start + 1 : odd_start + IMG], in_=channels[:, 1:IMG])
+            nc.gpsimd.tensor_copy(out=image[:, odd_start : odd_start + 2], in_=image[:, LEAD : LEAD + 2])
 
         zeros = keep.tile([P, H_OUT * 2], BF16, name="zeros")
         nc.vector.memset(zeros[:], 0.0)

@@ -24,108 +24,146 @@ GROUP_COLS = 2 * PART_ROWS * HALF
 
 BLOCK = 16
 LEAD = H + 1
-COPY_LEN = -(-(LEAD + 1 + IMG + H + 1) // BLOCK) * BLOCK
-COPY_WORDS = COPY_LEN // 2
-HEAD_END = -(-(LEAD + 1) // BLOCK) * BLOCK
-TAIL_START = (LEAD + IMG) // BLOCK * BLOCK
+PART_IMAGE_ROWS = H_OUT // PARTS
 
 FLOPS = 2 * BATCH * H_OUT * H_OUT * C_IN * PACK * C_OUT
 
 
-def word_of_pair(ip, jp, di):
+def copy_length(parts):
+    return -(-(LEAD + 1 + H * PART_IMAGE_ROWS * len(parts) + 1) // BLOCK) * BLOCK
+
+
+def word_of_pair(ip, jp, di, copy_words):
     element = LEAD + H * (ip + di - 1) + (jp - 1)
     odd = element % 2
-    return odd * COPY_WORDS + (element + odd) // 2
+    return odd * copy_words + (element + odd) // 2
 
 
 def tile_conv2d_s_kernel(tc, x, K, out):
     nc = tc.nc
     chunks = [(b, g) for b in range(BATCH) for g in range(PASSES)]
+    whole = tuple(range(PARTS))
+    pieces = [(chunks[0], (part,)) for part in whole] + [(chunk, whole) for chunk in chunks[1:]]
     with ExitStack() as ctx:
         keep = ctx.enter_context(tc.tile_pool(name="keep", bufs=1))
         banks = ctx.enter_context(tc.psum_pool(name="banks", bufs=1))
         ctx.enter_context(tc.manual_schedule())
 
+        zeros = keep.tile([P, H_OUT * 2], BF16, name="zeros")
+        nc.vector.memset(zeros[:], 0.0)
+        warm = keep.tile([P, 1], BF16, name="warm")
+        nc.scalar.copy(out=warm[:], in_=zeros[:, 0:1])
+
+        images = {}
+
+        def load_image(piece):
+            (b, g), parts = piece
+            length = copy_length(parts)
+            first = H * PART_IMAGE_ROWS * parts[0]
+            behind = first + H * PART_IMAGE_ROWS * len(parts) + 1
+            image = keep.tile([P, 3 * length], BF16, name="image_%d_%d_%d" % (b, g, parts[0]))
+            images[piece] = image
+            both = image[:, 0 : 2 * length].rearrange("q (v l) -> q v l", v=2)
+            channels = x[b, g * P : (g + 1) * P].rearrange("c h w -> c (h w)")
+            if behind > IMG:
+                nc.vector.memset(both[:, :, (LEAD + IMG - first) // BLOCK * BLOCK : length], 0.0)
+                behind = IMG
+            if first == 0:
+                nc.vector.memset(both[:, :, 0:LEAD], 0.0)
+                nc.sync.dma_start(out=image[:, LEAD : LEAD + behind], in_=channels[:, 0:behind])
+                nc.sync.dma_start(out=image[:, length + LEAD + 2 : length + LEAD + 1 + behind], in_=channels[:, 1:behind])
+                nc.gpsimd.tensor_copy(out=image[:, length + LEAD : length + LEAD + 3], in_=image[:, LEAD - 1 : LEAD + 2])
+            else:
+                nc.sync.dma_start(out=image[:, 0 : LEAD + behind - first], in_=channels[:, first - LEAD : behind])
+                nc.sync.dma_start(
+                    out=image[:, length : length + LEAD + 1 + behind - first], in_=channels[:, first - LEAD - 1 : behind]
+                )
+
+        load_image(pieces[0])
         k_rows = keep.tile([P, PASSES, PACK, C_OUT], BF16, name="k_rows")
         nc.sync.dma_start(
             out=k_rows[:].rearrange("q g t o -> q g (t o)"),
             in_=K.rearrange("kh kw c o -> (kh kw c) o").rearrange("(g q t) o -> q g (t o)", g=PASSES, q=P),
         )
-
-        images = {}
-        for b, g in chunks:
-            image = keep.tile([P, 3 * COPY_LEN], BF16, name="image_%d_%d" % (b, g))
-            images[(b, g)] = image
-            both = image[:, 0 : 2 * COPY_LEN].rearrange("q (v l) -> q v l", v=2)
-            nc.vector.memset(both[:, :, 0:HEAD_END], 0.0)
-            nc.vector.memset(both[:, :, TAIL_START:COPY_LEN], 0.0)
-            channels = x[b, g * P : (g + 1) * P].rearrange("c h w -> c (h w)")
-            odd_start = COPY_LEN + LEAD + 1
-            nc.sync.dma_start(out=image[:, LEAD : LEAD + IMG], in_=channels)
-            nc.sync.dma_start(out=image[:, odd_start + 1 : odd_start + IMG], in_=channels[:, 1:IMG])
-            nc.gpsimd.tensor_copy(out=image[:, odd_start : odd_start + 2], in_=image[:, LEAD : LEAD + 2])
-
-        zeros = keep.tile([P, H_OUT * 2], BF16, name="zeros")
-        nc.vector.memset(zeros[:], 0.0)
+        for piece in pieces[1:]:
+            load_image(piece)
 
         k_grouped = keep.tile([P, PASSES, C_OUT, PACK], BF16, name="k_grouped", align_bytes=64)
         k_codes = keep.tile([P, PASSES, C_OUT], U32, name="k_codes", align_bytes=64)
         k_scales = keep.tile([P, PASSES, C_OUT], U8, name="k_scales", align_bytes=64)
-        side_by_side = k_rows[:].rearrange("q g t o -> q g o t")
-        nc.vector.tensor_copy(out=k_grouped[:, 0], in_=side_by_side[:, 0])
-        nc.scalar.copy(out=k_grouped[:, 1], in_=side_by_side[:, 1])
-        nc.vector.quantize_mx(
-            out=k_codes[:].rearrange("q g o -> q (g o)").bitcast(FP8X4),
-            scales=k_scales[:].rearrange("q g o -> q (g o)"),
-            in_=k_grouped[:].rearrange("q g o t -> q (g o t)"),
-        )
 
-        def windows_of_class(image, ip, jp):
-            words = [word_of_pair(ip, jp, di) for di in range(2)]
+        def group_kf():
+            side_by_side = k_rows[:].rearrange("q g t o -> q g o t")
+            nc.vector.tensor_copy(out=k_grouped[:, 0], in_=side_by_side[:, 0])
+            nc.scalar.copy(out=k_grouped[:, 1], in_=side_by_side[:, 1])
+
+        def quantise_kf():
+            nc.vector.quantize_mx(
+                out=k_codes[:].rearrange("q g o -> q (g o)").bitcast(FP8X4),
+                scales=k_scales[:].rearrange("q g o -> q (g o)"),
+                in_=k_grouped[:].rearrange("q g o t -> q (g o t)"),
+            )
+
+        def windows_of_class(piece, ip, jp):
+            parts = piece[1]
+            words = [word_of_pair(ip, jp, di, copy_length(parts) // 2) for di in range(2)]
             start = min(words)
             apart = max(words) - start
-            two_rows = image[:].bitcast(F32)[:, start : start + 2 * apart].rearrange("q (d f) -> q d f", d=2)
+            two_rows = images[piece][:].bitcast(F32)[:, start : start + 2 * apart].rearrange("q (d f) -> q d f", d=2)
             if words[0] > words[1]:
                 two_rows = two_rows[:, ::-1]
-            grid = two_rows[:, :, 0 : HALF * H].rearrange("q d (a r) -> q d a r", r=H)[:, :, :, 0:HALF]
-            return grid.rearrange("q d (part a) m -> q part a m d", part=PARTS)
+            rows = PART_ROWS * len(parts)
+            grid = two_rows[:, :, 0 : rows * H].rearrange("q d (a r) -> q d a r", r=H)[:, :, :, 0:HALF]
+            return grid.rearrange("q d (part a) m -> q part a m d", part=len(parts))
 
         windows = {}
         p_codes = {}
         p_scales = {}
+        for chunk in chunks:
+            windows[chunk] = keep.tile([P, 2, PARTS, GROUP_COLS * PACK], BF16, name="windows_%d_%d" % chunk, align_bytes=64)
+            p_codes[chunk] = keep.tile([P, 2, PARTS, GROUP_COLS], U32, name="codes_%d_%d" % chunk, align_bytes=64)
+            p_scales[chunk] = keep.tile([P, 2, PARTS, GROUP_COLS], U8, name="scales_%d_%d" % chunk, align_bytes=64)
 
-        def build_windows(chunk):
-            tile = keep.tile([P, 2, PARTS, GROUP_COLS * PACK], BF16, name="windows_%d_%d" % chunk, align_bytes=64)
-            windows[chunk] = tile
-            pairs = tile[:].bitcast(F32).rearrange("q ip part (jp a m d) -> q ip jp part a m d", jp=2, a=PART_ROWS, m=HALF)
-            values = tile[:].rearrange(
-                "q ip part (jp a m d dj) -> q jp m dj (ip part) a d", jp=2, a=PART_ROWS, m=HALF, d=2
+        def build_windows(piece):
+            chunk, parts = piece
+            some = slice(parts[0], parts[0] + len(parts))
+            pairs = windows[chunk][:].bitcast(F32).rearrange(
+                "q ip part (jp a m d) -> q ip jp part a m d", jp=2, a=PART_ROWS, m=HALF
+            )
+            values = windows[chunk][:].rearrange(
+                "q ip part (jp a m d dj) -> q jp m dj ip part a d", jp=2, a=PART_ROWS, m=HALF, d=2
             )
             for ip in range(2):
-                nc.vector.tensor_copy(out=pairs[:, ip, 0], in_=windows_of_class(images[chunk], ip, 0))
-                nc.scalar.copy(out=pairs[:, ip, 1], in_=windows_of_class(images[chunk], ip, 1))
-            padding = zeros[:].rearrange("q (n a d) -> q n a d", a=PART_ROWS, d=2)
-            nc.scalar.copy(out=values[:, 0, 0, 0], in_=padding)
-            nc.scalar.copy(out=values[:, 1, HALF - 1, 1], in_=padding)
+                nc.vector.tensor_copy(out=pairs[:, ip, 0, some], in_=windows_of_class(piece, ip, 0))
+                nc.scalar.copy(out=pairs[:, ip, 1, some], in_=windows_of_class(piece, ip, 1))
+            count = 2 * len(parts)
+            padding = zeros[:, 0 : count * PART_ROWS * 2].rearrange("q (n a d) -> q n a d", a=PART_ROWS, d=2)
+            for jp, m, dj in ((0, 0, 0), (1, HALF - 1, 1)):
+                if len(parts) == PARTS:
+                    places = values[:, jp, m, dj].rearrange("q ip part a d -> q (ip part) a d")
+                else:
+                    places = values[:, jp, m, dj, :, parts[0]]
+                nc.scalar.copy(out=places, in_=padding)
 
-        def quantise_windows(chunk):
-            codes = keep.tile([P, 2, PARTS, GROUP_COLS], U32, name="codes_%d_%d" % chunk, align_bytes=64)
-            scales = keep.tile([P, 2, PARTS, GROUP_COLS], U8, name="scales_%d_%d" % chunk, align_bytes=64)
+        def quantise_windows(piece):
+            chunk, parts = piece
             for ip in range(2):
-                for part in range(PARTS):
+                for part in parts:
                     nc.vector.quantize_mx(
-                        out=codes[:, ip, part].bitcast(FP8X4),
-                        scales=scales[:, ip, part],
+                        out=p_codes[chunk][:, ip, part].bitcast(FP8X4),
+                        scales=p_scales[chunk][:, ip, part],
                         in_=windows[chunk][:, ip, part],
                     )
-            p_codes[chunk] = codes
-            p_scales[chunk] = scales
 
-        build_windows(chunks[0])
-        for n in range(1, len(chunks)):
-            build_windows(chunks[n])
-            quantise_windows(chunks[n - 1])
-        quantise_windows(chunks[-1])
+        build_windows(pieces[0])
+        group_kf()
+        build_windows(pieces[1])
+        quantise_kf()
+        quantise_windows(pieces[0])
+        for n in range(2, len(pieces)):
+            build_windows(pieces[n])
+            quantise_windows(pieces[n - 1])
+        quantise_windows(pieces[-1])
 
         for b in range(BATCH):
             result = keep.tile([P, H_OUT * H_OUT], F32, name="result_%d" % b)

@@ -18,19 +18,19 @@ H_OUT = 32
 IMG = H * H
 PASSES = C_IN // P
 HALF = H_OUT // 2
-PARTS = 2
-PART_ROWS = HALF // PARTS
-GROUP_COLS = 2 * PART_ROWS * HALF
+ROW_VALUES = HALF * PACK
+SIDE_COLS = H_OUT * HALF
+SIDE_VALUES = SIDE_COLS * PACK
+PADDING_STEP = SIDE_VALUES + (HALF - 1) * PACK + 1
 
 BLOCK = 16
 LEAD = H + 1
-PART_IMAGE_ROWS = H_OUT // PARTS
 
 FLOPS = 2 * BATCH * H_OUT * H_OUT * C_IN * PACK * C_OUT
 
 
-def copy_length(parts):
-    return -(-(LEAD + 1 + H * PART_IMAGE_ROWS * len(parts) + 1) // BLOCK) * BLOCK
+def copy_length(rows):
+    return -(-(LEAD + 1 + H * rows + 1) // BLOCK) * BLOCK
 
 
 def word_of_pair(ip, jp, di, copy_words):
@@ -42,34 +42,40 @@ def word_of_pair(ip, jp, di, copy_words):
 def tile_conv2d_s_kernel(tc, x, K, out):
     nc = tc.nc
     chunks = [(b, g) for b in range(BATCH) for g in range(PASSES)]
-    whole = tuple(range(PARTS))
-    pieces = [(chunks[0], (part,)) for part in whole] + [(chunk, whole) for chunk in chunks[1:]]
+    pieces = [(chunks[0], 0, HALF), (chunks[0], HALF, HALF)] + [(chunk, 0, H_OUT) for chunk in chunks[1:]]
+    units = {0: [(0, HALF), (HALF, H_OUT)], 1: [(0, HALF), (HALF, HALF + 8), (HALF + 8, H_OUT)]}
     with ExitStack() as ctx:
         keep = ctx.enter_context(tc.tile_pool(name="keep", bufs=1))
         banks = ctx.enter_context(tc.psum_pool(name="banks", bufs=1))
         ctx.enter_context(tc.manual_schedule())
 
-        zeros = keep.tile([P, H_OUT * 2], BF16, name="zeros")
+        zeros = keep.tile([P, H_OUT * PACK], BF16, name="zeros")
         nc.vector.memset(zeros[:], 0.0)
         warm = keep.tile([P, 1], BF16, name="warm")
         nc.scalar.copy(out=warm[:], in_=zeros[:, 0:1])
 
-        images = {}
+        def extent(piece):
+            first = H * piece[1]
+            return copy_length(piece[2]), first, first + H * piece[2] + 1
 
-        def load_image(piece):
-            (b, g), parts = piece
-            length = copy_length(parts)
-            first = H * PART_IMAGE_ROWS * parts[0]
-            behind = first + H * PART_IMAGE_ROWS * len(parts) + 1
-            image = keep.tile([P, 3 * length], BF16, name="image_%d_%d_%d" % (b, g, parts[0]))
+        images = {}
+        for piece in pieces:
+            length, first, behind = extent(piece)
+            image = keep.tile([P, 3 * length], BF16, name="image_%d_%d_%d" % (piece[0][0], piece[0][1], piece[1]))
             images[piece] = image
             both = image[:, 0 : 2 * length].rearrange("q (v l) -> q v l", v=2)
-            channels = x[b, g * P : (g + 1) * P].rearrange("c h w -> c (h w)")
             if behind > IMG:
                 nc.vector.memset(both[:, :, (LEAD + IMG - first) // BLOCK * BLOCK : length], 0.0)
-                behind = IMG
             if first == 0:
                 nc.vector.memset(both[:, :, 0:LEAD], 0.0)
+
+        def load_image(piece):
+            b, g = piece[0]
+            length, first, behind = extent(piece)
+            behind = min(behind, IMG)
+            image = images[piece]
+            channels = x[b, g * P : (g + 1) * P].rearrange("c h w -> c (h w)")
+            if first == 0:
                 nc.sync.dma_start(out=image[:, LEAD : LEAD + behind], in_=channels[:, 0:behind])
                 nc.sync.dma_start(out=image[:, length + LEAD + 2 : length + LEAD + 1 + behind], in_=channels[:, 1:behind])
                 nc.gpsimd.tensor_copy(out=image[:, length + LEAD : length + LEAD + 3], in_=image[:, LEAD - 1 : LEAD + 2])
@@ -93,9 +99,7 @@ def tile_conv2d_s_kernel(tc, x, K, out):
         k_scales = keep.tile([P, PASSES, C_OUT], U8, name="k_scales", align_bytes=64)
 
         def group_kf():
-            side_by_side = k_rows[:].rearrange("q g t o -> q g o t")
-            nc.vector.tensor_copy(out=k_grouped[:, 0], in_=side_by_side[:, 0])
-            nc.scalar.copy(out=k_grouped[:, 1], in_=side_by_side[:, 1])
+            nc.vector.tensor_copy(out=k_grouped[:], in_=k_rows[:].rearrange("q g t o -> q g o t"))
 
         def quantise_kf():
             nc.vector.quantize_mx(
@@ -105,55 +109,51 @@ def tile_conv2d_s_kernel(tc, x, K, out):
             )
 
         def windows_of_class(piece, ip, jp):
-            parts = piece[1]
-            words = [word_of_pair(ip, jp, di, copy_length(parts) // 2) for di in range(2)]
+            words = [word_of_pair(ip, jp, di, copy_length(piece[2]) // 2) for di in range(2)]
             start = min(words)
             apart = max(words) - start
             two_rows = images[piece][:].bitcast(F32)[:, start : start + 2 * apart].rearrange("q (d f) -> q d f", d=2)
             if words[0] > words[1]:
                 two_rows = two_rows[:, ::-1]
-            rows = PART_ROWS * len(parts)
-            grid = two_rows[:, :, 0 : rows * H].rearrange("q d (a r) -> q d a r", r=H)[:, :, :, 0:HALF]
-            return grid.rearrange("q d (part a) m -> q part a m d", part=len(parts))
+            grid = two_rows[:, :, 0 : piece[2] // 2 * H].rearrange("q d (a r) -> q d a r", r=H)[:, :, :, 0:HALF]
+            return grid.rearrange("q d a m -> q a m d")
 
         windows = {}
         p_codes = {}
         p_scales = {}
         for chunk in chunks:
-            windows[chunk] = keep.tile([P, 2, PARTS, GROUP_COLS * PACK], BF16, name="windows_%d_%d" % chunk, align_bytes=64)
-            p_codes[chunk] = keep.tile([P, 2, PARTS, GROUP_COLS], U32, name="codes_%d_%d" % chunk, align_bytes=64)
-            p_scales[chunk] = keep.tile([P, 2, PARTS, GROUP_COLS], U8, name="scales_%d_%d" % chunk, align_bytes=64)
+            windows[chunk] = keep.tile(
+                [P, -(-2 * PADDING_STEP // BLOCK) * BLOCK], BF16, name="windows_%d_%d" % chunk, align_bytes=64
+            )
+            p_codes[chunk] = keep.tile([P, 2, SIDE_COLS], U32, name="codes_%d_%d" % chunk, align_bytes=64)
+            p_scales[chunk] = keep.tile([P, 2, SIDE_COLS], U8, name="scales_%d_%d" % chunk, align_bytes=64)
 
         def build_windows(piece):
-            chunk, parts = piece
-            some = slice(parts[0], parts[0] + len(parts))
-            pairs = windows[chunk][:].bitcast(F32).rearrange(
-                "q ip part (jp a m d) -> q ip jp part a m d", jp=2, a=PART_ROWS, m=HALF
+            chunk, row, rows = piece
+            pairs = windows[chunk][:, 0 : 2 * SIDE_VALUES].bitcast(F32).rearrange(
+                "q (jp a ip m d) -> q jp ip a m d", jp=2, ip=2, m=HALF, d=2
             )
-            values = windows[chunk][:].rearrange(
-                "q ip part (jp a m d dj) -> q jp m dj ip part a d", jp=2, a=PART_ROWS, m=HALF, d=2
-            )
+            some = slice(row // 2, (row + rows) // 2)
             for ip in range(2):
-                nc.vector.tensor_copy(out=pairs[:, ip, 0, some], in_=windows_of_class(piece, ip, 0))
-                nc.scalar.copy(out=pairs[:, ip, 1, some], in_=windows_of_class(piece, ip, 1))
-            count = 2 * len(parts)
-            padding = zeros[:, 0 : count * PART_ROWS * 2].rearrange("q (n a d) -> q n a d", a=PART_ROWS, d=2)
-            for jp, m, dj in ((0, 0, 0), (1, HALF - 1, 1)):
-                if len(parts) == PARTS:
-                    places = values[:, jp, m, dj].rearrange("q ip part a d -> q (ip part) a d")
-                else:
-                    places = values[:, jp, m, dj, :, parts[0]]
-                nc.scalar.copy(out=places, in_=padding)
+                nc.vector.tensor_copy(out=pairs[:, 0, ip, some], in_=windows_of_class(piece, ip, 0))
+                nc.scalar.copy(out=pairs[:, 1, ip, some], in_=windows_of_class(piece, ip, 1))
+            sides = windows[chunk][:, 0 : 2 * PADDING_STEP].rearrange("q (s v) -> q s v", s=2)
+            places = sides[:, :, row * ROW_VALUES : (row + rows) * ROW_VALUES].rearrange("q s (i v) -> q s i v", v=ROW_VALUES)
+            for side in range(2):
+                nc.scalar.copy(
+                    out=places[:, side, :, 0:PACK:2], in_=zeros[:, 0 : rows * 2].rearrange("q (i d) -> q i d", d=2)
+                )
 
         def quantise_windows(piece):
-            chunk, parts = piece
-            for ip in range(2):
-                for part in parts:
-                    nc.vector.quantize_mx(
-                        out=p_codes[chunk][:, ip, part].bitcast(FP8X4),
-                        scales=p_scales[chunk][:, ip, part],
-                        in_=windows[chunk][:, ip, part],
-                    )
+            chunk, row, rows = piece
+            for start, end in units[chunk[0]]:
+                if row <= start < row + rows:
+                    for jp in range(2):
+                        nc.vector.quantize_mx(
+                            out=p_codes[chunk][:, jp, start * HALF : end * HALF].bitcast(FP8X4),
+                            scales=p_scales[chunk][:, jp, start * HALF : end * HALF],
+                            in_=windows[chunk][:, jp * SIDE_VALUES + start * ROW_VALUES : jp * SIDE_VALUES + end * ROW_VALUES],
+                        )
 
         build_windows(pieces[0])
         group_kf()
@@ -167,23 +167,21 @@ def tile_conv2d_s_kernel(tc, x, K, out):
 
         for b in range(BATCH):
             result = keep.tile([P, H_OUT * H_OUT], F32, name="result_%d" % b)
-            rows = result[:].rearrange("o (part a ip m jp) -> o ip part a m jp", part=PARTS, a=PART_ROWS, ip=2, m=HALF)
-            for ip in range(2):
-                for part in range(PARTS):
-                    acc = banks.tile([P, GROUP_COLS], F32, name="acc_%d_%d_%d" % (b, ip, part))
+            for start, end in units[b]:
+                acc = banks.tile([P, 2, (end - start) * HALF], F32, name="acc_%d_%d" % (b, start))
+                for jp in range(2):
                     for g in range(PASSES):
                         nc.tensor.matmul_mx(
-                            out=acc[:],
+                            out=acc[:, jp],
                             lhsT=k_codes[:, g].bitcast(FP8X4),
                             lhsT_scale=k_scales[:, g],
-                            rhs=p_codes[(b, g)][:, ip, part].bitcast(FP8X4),
-                            rhs_scale=p_scales[(b, g)][:, ip, part],
+                            rhs=p_codes[(b, g)][:, jp, start * HALF : end * HALF].bitcast(FP8X4),
+                            rhs_scale=p_scales[(b, g)][:, jp, start * HALF : end * HALF],
                             start=(g == 0),
                             stop=(g == PASSES - 1),
                         )
-                    nc.scalar.copy(
-                        out=rows[:, ip, part], in_=acc[:].rearrange("o (jp a m) -> o a m jp", jp=2, a=PART_ROWS)
-                    )
-            for part in range(PARTS):
-                some = slice(part * (H_OUT * HALF), (part + 1) * (H_OUT * HALF))
+                some = slice(start * H_OUT, end * H_OUT)
+                nc.scalar.copy(
+                    out=result[:, some].rearrange("o (n jp) -> o n jp", jp=2), in_=acc[:].rearrange("o jp n -> o n jp")
+                )
                 nc.sync.dma_start(out=out[b].rearrange("o i j -> o (i j)")[:, some], in_=result[:, some])

@@ -146,6 +146,13 @@ def tile_conv2d_s_kernel(tc, x, K, out):
 
         def quantise_windows(piece):
             chunk, row, rows = piece
+            if rows == H_OUT and chunk != chunks[-1]:
+                nc.vector.quantize_mx(
+                    out=p_codes[chunk][:].rearrange("q jp n -> q (jp n)").bitcast(FP8X4),
+                    scales=p_scales[chunk][:].rearrange("q jp n -> q (jp n)"),
+                    in_=windows[chunk][:, 0 : 2 * SIDE_VALUES],
+                )
+                return
             for start, end in units[chunk[0]]:
                 if row <= start < row + rows:
                     for jp in range(2):

@@ -36,7 +36,7 @@ def copy_length(rows):
 def word_of_pair(ip, jp, di, copy_words):
     element = LEAD + H * (ip + di - 1) + (jp - 1)
     odd = element % 2
-    return odd * copy_words + (element + odd) // 2
+    return (1 - odd) * copy_words + (element + odd) // 2
 
 
 def tile_conv2d_s_kernel(tc, x, K, out):
@@ -76,14 +76,14 @@ def tile_conv2d_s_kernel(tc, x, K, out):
             image = images[piece]
             channels = x[b, g * P : (g + 1) * P].rearrange("c h w -> c (h w)")
             if first == 0:
-                nc.sync.dma_start(out=image[:, LEAD : LEAD + behind], in_=channels[:, 0:behind])
-                nc.sync.dma_start(out=image[:, length + LEAD + 2 : length + LEAD + 1 + behind], in_=channels[:, 1:behind])
-                nc.gpsimd.tensor_copy(out=image[:, length + LEAD : length + LEAD + 3], in_=image[:, LEAD - 1 : LEAD + 2])
+                nc.sync.dma_start(out=image[:, length + LEAD : length + LEAD + behind], in_=channels[:, 0:behind])
+                nc.sync.dma_start(out=image[:, LEAD + 2 : LEAD + 1 + behind], in_=channels[:, 1:behind])
+                nc.gpsimd.tensor_copy(out=image[:, LEAD : LEAD + 3], in_=image[:, length + LEAD - 1 : length + LEAD + 2])
             else:
-                nc.sync.dma_start(out=image[:, 0 : LEAD + behind - first], in_=channels[:, first - LEAD : behind])
                 nc.sync.dma_start(
-                    out=image[:, length : length + LEAD + 1 + behind - first], in_=channels[:, first - LEAD - 1 : behind]
+                    out=image[:, length : length + LEAD + behind - first], in_=channels[:, first - LEAD : behind]
                 )
+                nc.sync.dma_start(out=image[:, 0 : LEAD + 1 + behind - first], in_=channels[:, first - LEAD - 1 : behind])
 
         load_image(pieces[0])
         k_rows = keep.tile([P, PASSES, PACK, C_OUT], BF16, name="k_rows")
@@ -136,7 +136,7 @@ def tile_conv2d_s_kernel(tc, x, K, out):
             some = slice(row // 2, (row + rows) // 2)
             for ip in range(2):
                 nc.vector.tensor_copy(out=pairs[:, 0, ip, some], in_=windows_of_class(piece, ip, 0))
-                nc.scalar.copy(out=pairs[:, 1, ip, some], in_=windows_of_class(piece, ip, 1))
+                nc.scalar.copy(out=pairs[:, 1, 1 - ip, some], in_=windows_of_class(piece, 1 - ip, 1))
             sides = windows[chunk][:, 0 : 2 * PADDING_STEP].rearrange("q (s v) -> q s v", s=2)
             places = sides[:, :, row * ROW_VALUES : (row + rows) * ROW_VALUES].rearrange("q s (i v) -> q s i v", v=ROW_VALUES)
             for side in range(2):

@@ -11,184 +11,182 @@ FP8X4 = mybir.dt.float8_e4m3fn_x4
 P = 128
 PACK = 4
 BATCH = 2
-C_IN = 256
 C_OUT = 128
 H = 31
 H_OUT = 32
 IMG = H * H
-PASSES = C_IN // P
+HALVES = 2
+U = P // HALVES
+PAIR = 2
+DI = 2
+DJ = 2
 HALF = H_OUT // 2
-ROW_VALUES = HALF * PACK
-SIDE_COLS = H_OUT * HALF
-SIDE_VALUES = SIDE_COLS * PACK
-PADDING_STEP = SIDE_VALUES + (HALF - 1) * PACK + 1
+ROW_WORDS = H_OUT * PAIR
+ROW_VALUES = ROW_WORDS * DJ
+WINDOW_ROWS = H_OUT + 1
+INNER = HALF - 1
 
-BLOCK = 16
-LEAD = H + 1
-
-FLOPS = 2 * BATCH * H_OUT * H_OUT * C_IN * PACK * C_OUT
-
-
-def copy_length(rows):
-    return -(-(LEAD + 1 + H * rows + 1) // BLOCK) * BLOCK
-
-
-def word_of_pair(ip, jp, di, copy_words):
-    element = LEAD + H * (ip + di - 1) + (jp - 1)
-    odd = element % 2
-    return (1 - odd) * copy_words + (element + odd) // 2
+FLOPS = 2 * BATCH * H_OUT * H_OUT * 256 * PACK * C_OUT
 
 
 def tile_conv2d_s_kernel(tc, x, K, out):
     nc = tc.nc
-    chunks = [(b, g) for b in range(BATCH) for g in range(PASSES)]
-    pieces = [(chunks[0], 0, HALF), (chunks[0], HALF, HALF)] + [(chunk, 0, H_OUT) for chunk in chunks[1:]]
-    units = {0: [(0, HALF), (HALF, H_OUT)], 1: [(0, HALF), (HALF, HALF + 8), (HALF + 8, H_OUT)]}
+    pieces = [(0, 0, 16), (0, 16, 15), (1, 0, 16), (1, 16, 15)]
+    units = [[(0, 16)], [(16, 32)], [(0, 16)], [(16, 24), (24, 32)]]
     with ExitStack() as ctx:
         keep = ctx.enter_context(tc.tile_pool(name="keep", bufs=1))
         banks = ctx.enter_context(tc.psum_pool(name="banks", bufs=1))
         ctx.enter_context(tc.manual_schedule())
 
-        zeros = keep.tile([P, H_OUT * PACK], BF16, name="zeros")
-        nc.vector.memset(zeros[:], 0.0)
+        k_rows = keep.tile([P, PAIR, DI * DJ * C_OUT], BF16, name="k_rows")
+        k_grouped = keep.tile([P, DI, C_OUT, PAIR, DJ], BF16, name="k_grouped", align_bytes=64)
+        k_codes = keep.tile([P, DI, C_OUT], U32, name="k_codes", align_bytes=64)
+        k_scales = keep.tile([P, DI, C_OUT], U8, name="k_scales", align_bytes=64)
+
+        lane = 2 * 272
+        images = []
+        for n in range(len(pieces)):
+            images.append(keep.tile([P, 2 * PAIR * lane], BF16, name="image_%d" % n))
+        windows = []
+        p_codes = {}
+        p_scales = {}
+        for b in range(BATCH):
+            windows.append(keep.tile([P, WINDOW_ROWS * ROW_VALUES], BF16, name="windows_%d" % b, align_bytes=64))
+            for di in range(DI):
+                p_codes[b, di] = keep.tile([P, H_OUT * H_OUT], U32, name="codes_%d_%d" % (b, di), align_bytes=64)
+                p_scales[b, di] = keep.tile([P, H_OUT * H_OUT], U8, name="scales_%d_%d" % (b, di), align_bytes=64)
+
+        queues = [nc.sync, nc.scalar]
+        k_halves = K.rearrange("kh kw c o -> (kh kw c) o").rearrange("(h e u t) o -> h u e (t o)", h=HALVES, e=PAIR, t=DI * DJ)
+
+        def load_k():
+            for h in range(HALVES):
+                queues[h].dma_start(out=k_rows[h * U : (h + 1) * U], in_=k_halves[h])
+
+        def load_image(n):
+            b, first, rows = pieces[n]
+            channels = x[b].rearrange("(h e u) i j -> h u e (i j)", h=HALVES, e=PAIR)
+            lanes = images[n][:].rearrange("q (v e l) -> q v e l", v=2, e=PAIR)
+            for v in range(2):
+                for h in range(HALVES):
+                    queues[h].dma_start(
+                        out=lanes[h * U : (h + 1) * U, v, :, 0 : rows * H - v],
+                        in_=channels[h][:, :, first * H + v : (first + rows) * H],
+                    )
+
+        load_k()
+        load_image(0)
+
+        zeros = keep.tile([P, 1], BF16, name="zeros")
         warm = keep.tile([P, 1], BF16, name="warm")
-        nc.scalar.copy(out=warm[:], in_=zeros[:, 0:1])
+        nc.vector.memset(zeros[:], 0.0)
+        nc.scalar.copy(out=warm[:], in_=zeros[:])
+        load_image(1)
+        for b in range(BATCH):
+            words = windows[b][:].bitcast(F32)
+            nc.vector.memset(words[:, 0:ROW_WORDS], 0.0)
+            nc.vector.memset(words[:, (WINDOW_ROWS - 1) * ROW_WORDS :], 0.0)
+            edges = words[:, ROW_WORDS - 2 : ROW_WORDS - 2 + H_OUT * ROW_WORDS].rearrange("q (w f) -> q w f", f=ROW_WORDS)
+            nc.vector.memset(edges[:, :, 0 : 2 * PAIR], 0.0)
 
-        def extent(piece):
-            first = H * piece[1]
-            return copy_length(piece[2]), first, first + H * piece[2] + 1
+        def build_class(engine_copy, n, ip, odd):
+            b, first, rows = pieces[n]
+            count = (rows - ip + 1) // 2
+            words = windows[b][:].bitcast(F32).rearrange("q (w f) -> q w f", f=ROW_WORDS)
+            start = H_OUT if odd else PAIR
+            to = words[:, first + 1 + ip : first + 1 + rows : 2, start : start + INNER * PAIR]
+            copy = (ip + 1 - odd) % 2
+            lanes = images[n][:].bitcast(F32).rearrange("q (v e l) -> q v e l", v=2, e=PAIR)
+            at = [0, 15 if odd else 16][ip]
+            grid = lanes[:, copy, :, at : at + count * H].rearrange("q e (a r) -> q e a r", r=H)[:, :, :, 0:INNER]
+            engine_copy(out=to.rearrange("q a (k e) -> q a k e", e=PAIR), in_=grid.rearrange("q e a k -> q a k e"))
 
-        images = {}
-        for piece in pieces:
-            length, first, behind = extent(piece)
-            image = keep.tile([P, 3 * length], BF16, name="image_%d_%d_%d" % (piece[0][0], piece[0][1], piece[1]))
-            images[piece] = image
-            both = image[:, 0 : 2 * length].rearrange("q (v l) -> q v l", v=2)
-            if behind > IMG:
-                nc.vector.memset(both[:, :, (LEAD + IMG - first) // BLOCK * BLOCK : length], 0.0)
-            if first == 0:
-                nc.vector.memset(both[:, :, 0:LEAD], 0.0)
+        def build_edges(engine_copy, n):
+            b, first, rows = pieces[n]
+            values = windows[b][:].rearrange("q (w f) -> q w f", f=ROW_VALUES)[:, first + 1 : first + 1 + rows]
+            grid = images[n][:].rearrange("q (v e l) -> q v e l", v=2, e=PAIR)[:, 0, :, 0 : rows * H]
+            grid = grid.rearrange("q e (i r) -> q i e r", r=H)
+            engine_copy(out=values[:, :, 1:4:2], in_=grid[:, :, :, 0])
+            engine_copy(out=values[:, :, ROW_VALUES - 4 : ROW_VALUES - 1 : 2], in_=grid[:, :, :, H - 1])
 
-        def load_image(piece):
-            b, g = piece[0]
-            length, first, behind = extent(piece)
-            behind = min(behind, IMG)
-            image = images[piece]
-            channels = x[b, g * P : (g + 1) * P].rearrange("c h w -> c (h w)")
-            if first == 0:
-                nc.sync.dma_start(out=image[:, length + LEAD : length + LEAD + behind], in_=channels[:, 0:behind])
-                nc.sync.dma_start(out=image[:, LEAD + 2 : LEAD + 1 + behind], in_=channels[:, 1:behind])
-                nc.gpsimd.tensor_copy(out=image[:, LEAD : LEAD + 3], in_=image[:, length + LEAD - 1 : length + LEAD + 2])
-            else:
-                nc.sync.dma_start(
-                    out=image[:, length : length + LEAD + behind - first], in_=channels[:, first - LEAD : behind]
+        def quantise(n, start, end, di):
+            b = pieces[n][0]
+            nc.vector.quantize_mx(
+                out=p_codes[b, di][:, start * H_OUT : end * H_OUT].bitcast(FP8X4),
+                scales=p_scales[b, di][:, start * H_OUT : end * H_OUT],
+                in_=windows[b][:, (start + di) * ROW_VALUES : (end + di) * ROW_VALUES],
+            )
+
+        results = []
+        for b in range(BATCH):
+            results.append(keep.tile([P, H_OUT * H_OUT], F32, name="result_%d" % b))
+
+        pending = []
+
+        def products(n):
+            b = pieces[n][0]
+            for start, end in units[n]:
+                acc = banks.tile([P, (end - start) * H_OUT], F32, name="acc_%d_%d" % (b, start))
+                some = slice(start * H_OUT, end * H_OUT)
+                for di in range(DI):
+                    nc.tensor.matmul_mx(
+                        out=acc[:],
+                        lhsT=k_codes[:, di].bitcast(FP8X4),
+                        lhsT_scale=k_scales[:, di],
+                        rhs=p_codes[b, di][:, some].bitcast(FP8X4),
+                        rhs_scale=p_scales[b, di][:, some],
+                        start=(di == 0),
+                        stop=(di == DI - 1),
+                    )
+                pending.append((b, start, end, acc))
+
+        def leave(b, start, end, acc):
+                some = slice(start * H_OUT, end * H_OUT)
+                nc.scalar.copy(
+                    out=results[b][:, some].rearrange("o (i m jp) -> o i m jp", m=HALF, jp=2),
+                    in_=acc[:].rearrange("o (i jp m) -> o i m jp", jp=2, m=HALF),
                 )
-                nc.sync.dma_start(out=image[:, 0 : LEAD + 1 + behind - first], in_=channels[:, first - LEAD - 1 : behind])
+                nc.sync.dma_start(out=out[b].rearrange("o i j -> o (i j)")[:, some], in_=results[b][:, some])
 
-        load_image(pieces[0])
-        k_rows = keep.tile([P, PASSES, PACK, C_OUT], BF16, name="k_rows")
-        nc.sync.dma_start(
-            out=k_rows[:].rearrange("q g t o -> q g (t o)"),
-            in_=K.rearrange("kh kw c o -> (kh kw c) o").rearrange("(g q t) o -> q g (t o)", g=PASSES, q=P),
-        )
-        for piece in pieces[1:]:
-            load_image(piece)
-
-        k_grouped = keep.tile([P, PASSES, C_OUT, PACK], BF16, name="k_grouped", align_bytes=64)
-        k_codes = keep.tile([P, PASSES, C_OUT], U32, name="k_codes", align_bytes=64)
-        k_scales = keep.tile([P, PASSES, C_OUT], U8, name="k_scales", align_bytes=64)
-
-        def group_kf():
-            nc.vector.tensor_copy(out=k_grouped[:], in_=k_rows[:].rearrange("q g t o -> q g o t"))
-
-        def quantise_kf():
+        def group_k():
+            for di in range(DI):
+                nc.vector.tensor_copy(
+                    out=k_grouped[:, di],
+                    in_=k_rows[:, :, di * DJ * C_OUT : (di + 1) * DJ * C_OUT].rearrange("q e (t o) -> q o e t", t=DJ),
+                )
             nc.vector.quantize_mx(
                 out=k_codes[:].rearrange("q g o -> q (g o)").bitcast(FP8X4),
                 scales=k_scales[:].rearrange("q g o -> q (g o)"),
-                in_=k_grouped[:].rearrange("q g o t -> q (g o t)"),
+                in_=k_grouped[:].rearrange("q g o e t -> q (g o e t)"),
             )
 
-        def windows_of_class(piece, ip, jp):
-            words = [word_of_pair(ip, jp, di, copy_length(piece[2]) // 2) for di in range(2)]
-            start = min(words)
-            apart = max(words) - start
-            two_rows = images[piece][:].bitcast(F32)[:, start : start + 2 * apart].rearrange("q (d f) -> q d f", d=2)
-            if words[0] > words[1]:
-                two_rows = two_rows[:, ::-1]
-            grid = two_rows[:, :, 0 : piece[2] // 2 * H].rearrange("q d (a r) -> q d a r", r=H)[:, :, :, 0:HALF]
-            return grid.rearrange("q d a m -> q a m d")
+        group_k()
 
-        windows = {}
-        p_codes = {}
-        p_scales = {}
-        for chunk in chunks:
-            windows[chunk] = keep.tile(
-                [P, -(-2 * PADDING_STEP // BLOCK) * BLOCK], BF16, name="windows_%d_%d" % chunk, align_bytes=64
-            )
-            p_codes[chunk] = keep.tile([P, 2, SIDE_COLS], U32, name="codes_%d_%d" % chunk, align_bytes=64)
-            p_scales[chunk] = keep.tile([P, 2, SIDE_COLS], U8, name="scales_%d_%d" % chunk, align_bytes=64)
+        def build_scalar(n):
+            build_class(nc.scalar.copy, n, 0, 1)
+            build_class(nc.scalar.copy, n, 1, 0)
+            build_edges(nc.scalar.copy, n)
+            build_class(nc.scalar.copy, n, 0, 0)
 
-        def build_windows(piece):
-            chunk, row, rows = piece
-            pairs = windows[chunk][:, 0 : 2 * SIDE_VALUES].bitcast(F32).rearrange(
-                "q (jp a ip m d) -> q jp ip a m d", jp=2, ip=2, m=HALF, d=2
-            )
-            some = slice(row // 2, (row + rows) // 2)
-            for ip in range(2):
-                nc.vector.tensor_copy(out=pairs[:, 0, ip, some], in_=windows_of_class(piece, ip, 0))
-                nc.scalar.copy(out=pairs[:, 1, 1 - ip, some], in_=windows_of_class(piece, 1 - ip, 1))
-            sides = windows[chunk][:, 0 : 2 * PADDING_STEP].rearrange("q (s v) -> q s v", s=2)
-            places = sides[:, :, row * ROW_VALUES : (row + rows) * ROW_VALUES].rearrange("q s (i v) -> q s i v", v=ROW_VALUES)
-            for side in range(2):
-                nc.scalar.copy(
-                    out=places[:, side, :, 0:PACK:2], in_=zeros[:, 0 : rows * 2].rearrange("q (i d) -> q i d", d=2)
-                )
+        def build_vector(n):
+            build_class(nc.vector.tensor_copy, n, 1, 1)
 
-        def quantise_windows(piece):
-            chunk, row, rows = piece
-            if rows == H_OUT and chunk != chunks[-1]:
-                nc.vector.quantize_mx(
-                    out=p_codes[chunk][:].rearrange("q jp n -> q (jp n)").bitcast(FP8X4),
-                    scales=p_scales[chunk][:].rearrange("q jp n -> q (jp n)"),
-                    in_=windows[chunk][:, 0 : 2 * SIDE_VALUES],
-                )
-                return
-            for start, end in units[chunk[0]]:
-                if row <= start < row + rows:
-                    for jp in range(2):
-                        nc.vector.quantize_mx(
-                            out=p_codes[chunk][:, jp, start * HALF : end * HALF].bitcast(FP8X4),
-                            scales=p_scales[chunk][:, jp, start * HALF : end * HALF],
-                            in_=windows[chunk][:, jp * SIDE_VALUES + start * ROW_VALUES : jp * SIDE_VALUES + end * ROW_VALUES],
-                        )
-
-        build_windows(pieces[0])
-        group_kf()
-        build_windows(pieces[1])
-        quantise_kf()
-        quantise_windows(pieces[0])
-        for n in range(2, len(pieces)):
-            build_windows(pieces[n])
-            quantise_windows(pieces[n - 1])
-        quantise_windows(pieces[-1])
-
-        for b in range(BATCH):
-            result = keep.tile([P, H_OUT * H_OUT], F32, name="result_%d" % b)
-            for start, end in units[b]:
-                acc = banks.tile([P, 2, (end - start) * HALF], F32, name="acc_%d_%d" % (b, start))
-                for jp in range(2):
-                    for g in range(PASSES):
-                        nc.tensor.matmul_mx(
-                            out=acc[:, jp],
-                            lhsT=k_codes[:, g].bitcast(FP8X4),
-                            lhsT_scale=k_scales[:, g],
-                            rhs=p_codes[(b, g)][:, jp, start * HALF : end * HALF].bitcast(FP8X4),
-                            rhs_scale=p_scales[(b, g)][:, jp, start * HALF : end * HALF],
-                            start=(g == 0),
-                            stop=(g == PASSES - 1),
-                        )
-                some = slice(start * H_OUT, end * H_OUT)
-                nc.scalar.copy(
-                    out=result[:, some].rearrange("o (n jp) -> o n jp", jp=2), in_=acc[:].rearrange("o jp n -> o n jp")
-                )
-                nc.sync.dma_start(out=out[b].rearrange("o i j -> o (i j)")[:, some], in_=result[:, some])
+        build_vector(0)
+        build_scalar(0)
+        load_image(2)
+        build_scalar(1)
+        load_image(3)
+        for n in range(len(pieces)):
+            first_calls = True
+            for start, end in units[n]:
+                quantise(n, start, end, 0)
+                if first_calls and n + 1 < len(pieces):
+                    build_vector(n + 1)
+                first_calls = False
+                quantise(n, start, end, 1)
+            if n + 2 < len(pieces):
+                build_scalar(n + 2)
+            products(n)
+            for item in pending:
+                leave(*item)
+            pending.clear()

@@ -14,14 +14,12 @@ BATCH = 2
 C_OUT = 128
 H = 31
 H_OUT = 32
-IMG = H * H
-HALVES = 2
-U = P // HALVES
-PAIR = 2
+HALFP = P // 2
+LANES = 2
 DI = 2
 DJ = 2
 HALF = H_OUT // 2
-ROW_WORDS = H_OUT * PAIR
+ROW_WORDS = H_OUT * LANES
 ROW_VALUES = ROW_WORDS * DJ
 WINDOW_ROWS = H_OUT + 1
 INNER = HALF - 1
@@ -32,21 +30,22 @@ FLOPS = 2 * BATCH * H_OUT * H_OUT * 256 * PACK * C_OUT
 def tile_conv2d_s_kernel(tc, x, K, out):
     nc = tc.nc
     pieces = [(0, 0, 16), (0, 16, 15), (1, 0, 16), (1, 16, 15)]
-    units = [[(0, 16)], [(16, 32)], [(0, 16)], [(16, 24), (24, 32)]]
+    groups = [(0, 0, 16), (1, 16, 15), (2, 0, 16), (3, 16, 15)]
+    units = [(0, 0, 16), (0, 16, 32), (1, 0, 16), (1, 16, 24), (1, 24, 32)]
     with ExitStack() as ctx:
         keep = ctx.enter_context(tc.tile_pool(name="keep", bufs=1))
         banks = ctx.enter_context(tc.psum_pool(name="banks", bufs=1))
         ctx.enter_context(tc.manual_schedule())
 
-        k_rows = keep.tile([P, PAIR, DI * DJ * C_OUT], BF16, name="k_rows")
-        k_grouped = keep.tile([P, DI, C_OUT, PAIR, DJ], BF16, name="k_grouped", align_bytes=64)
+        k_rows = keep.tile([P, LANES, DI * DJ * C_OUT], BF16, name="k_rows")
+        k_grouped = keep.tile([P, DI, C_OUT, LANES, DJ], BF16, name="k_grouped", align_bytes=64)
         k_codes = keep.tile([P, DI, C_OUT], U32, name="k_codes", align_bytes=64)
         k_scales = keep.tile([P, DI, C_OUT], U8, name="k_scales", align_bytes=64)
 
-        lane = 2 * 272
+        lengths = [-(-(H * rows + 64) // 16) * 16 for b, first, rows in pieces]
         images = []
         for n in range(len(pieces)):
-            images.append(keep.tile([P, 2 * PAIR * lane], BF16, name="image_%d" % n))
+            images.append(keep.tile([P, 2 * LANES * lengths[n]], BF16, name="image_%d" % n))
         windows = []
         p_codes = {}
         p_scales = {}
@@ -56,61 +55,65 @@ def tile_conv2d_s_kernel(tc, x, K, out):
                 p_codes[b, di] = keep.tile([P, H_OUT * H_OUT], U32, name="codes_%d_%d" % (b, di), align_bytes=64)
                 p_scales[b, di] = keep.tile([P, H_OUT * H_OUT], U8, name="scales_%d_%d" % (b, di), align_bytes=64)
 
-        queues = [nc.sync, nc.scalar]
-        k_halves = K.rearrange("kh kw c o -> (kh kw c) o").rearrange("(h e u t) o -> h u e (t o)", h=HALVES, e=PAIR, t=DI * DJ)
+        def load_lanes(to, channels):
+            nc.sync.dma_start(out=to[:, 0], in_=channels[HALFP : HALFP + P])
+            nc.sync.dma_start(out=to[0:HALFP, 1], in_=channels[0:HALFP])
+            nc.scalar.dma_start(out=to[HALFP:P, 1], in_=channels[P + HALFP : 2 * P])
 
         def load_k():
-            for h in range(HALVES):
-                queues[h].dma_start(out=k_rows[h * U : (h + 1) * U], in_=k_halves[h])
+            load_lanes(k_rows, K.rearrange("kh kw c o -> (kh kw c) o").rearrange("(c t) o -> c (t o)", t=DI * DJ))
 
         def load_image(n):
             b, first, rows = pieces[n]
-            channels = x[b].rearrange("(h e u) i j -> h u e (i j)", h=HALVES, e=PAIR)
-            lanes = images[n][:].rearrange("q (v e l) -> q v e l", v=2, e=PAIR)
-            for v in range(2):
-                for h in range(HALVES):
-                    queues[h].dma_start(
-                        out=lanes[h * U : (h + 1) * U, v, :, 0 : rows * H - v],
-                        in_=channels[h][:, :, first * H + v : (first + rows) * H],
-                    )
+            lanes = images[n][:].rearrange("q (v e l) -> q v e l", v=2, e=LANES)
+            channels = x[b].rearrange("c i j -> c (i j)")[:, first * H : (first + rows) * H]
+            load_lanes(lanes[:, 0, :, 0 : rows * H], channels)
+            nc.sync.dma_start(out=lanes[:, 1, 0, 0 : rows * H - 1], in_=channels[HALFP : HALFP + P, 1:])
 
-        load_k()
-        load_image(0)
+        def make_odd(n):
+            rows = pieces[n][2]
+            lanes = images[n][:].rearrange("q (v e l) -> q v e l", v=2, e=LANES)
+            nc.vector.tensor_copy(out=lanes[:, 1, 1, 0 : rows * H - 1], in_=lanes[:, 0, 1, 1 : rows * H])
 
-        zeros = keep.tile([P, 1], BF16, name="zeros")
-        warm = keep.tile([P, 1], BF16, name="warm")
-        nc.vector.memset(zeros[:], 0.0)
-        nc.scalar.copy(out=warm[:], in_=zeros[:])
-        load_image(1)
-        for b in range(BATCH):
+        def clear(b):
             words = windows[b][:].bitcast(F32)
             nc.vector.memset(words[:, 0:ROW_WORDS], 0.0)
             nc.vector.memset(words[:, (WINDOW_ROWS - 1) * ROW_WORDS :], 0.0)
             edges = words[:, ROW_WORDS - 2 : ROW_WORDS - 2 + H_OUT * ROW_WORDS].rearrange("q (w f) -> q w f", f=ROW_WORDS)
-            nc.vector.memset(edges[:, :, 0 : 2 * PAIR], 0.0)
+            nc.vector.memset(edges[:, :, 0 : 2 * LANES], 0.0)
 
-        def build_class(engine_copy, n, ip, odd):
-            b, first, rows = pieces[n]
+        def warm_up():
+            zeros = keep.tile([P, 1], BF16, name="zeros")
+            warm = keep.tile([P, 1], BF16, name="warm")
+            nc.vector.memset(zeros[:], 0.0)
+            nc.scalar.copy(out=warm[:], in_=zeros[:])
+
+        def build_class(engine_copy, g, ip, odd):
+            n, first, rows = groups[g]
+            b = pieces[n][0]
+            local = first - pieces[n][1]
             count = (rows - ip + 1) // 2
             words = windows[b][:].bitcast(F32).rearrange("q (w f) -> q w f", f=ROW_WORDS)
-            start = H_OUT if odd else PAIR
-            to = words[:, first + 1 + ip : first + 1 + rows : 2, start : start + INNER * PAIR]
+            start = H_OUT if odd else LANES
+            to = words[:, first + 1 + ip : first + 1 + rows : 2, start : start + INNER * LANES]
             copy = (ip + 1 - odd) % 2
-            lanes = images[n][:].bitcast(F32).rearrange("q (v e l) -> q v e l", v=2, e=PAIR)
-            at = [0, 15 if odd else 16][ip]
+            lanes = images[n][:].bitcast(F32).rearrange("q (v e l) -> q v e l", v=2, e=LANES)
+            at = local * H // 2 + [0, 15 if odd else 16][ip]
             grid = lanes[:, copy, :, at : at + count * H].rearrange("q e (a r) -> q e a r", r=H)[:, :, :, 0:INNER]
-            engine_copy(out=to.rearrange("q a (k e) -> q a k e", e=PAIR), in_=grid.rearrange("q e a k -> q a k e"))
+            engine_copy(out=to.rearrange("q a (k e) -> q a k e", e=LANES), in_=grid.rearrange("q e a k -> q a k e"))
 
-        def build_edges(engine_copy, n):
-            b, first, rows = pieces[n]
+        def build_edges(engine_copy, g):
+            n, first, rows = groups[g]
+            b = pieces[n][0]
+            local = first - pieces[n][1]
             values = windows[b][:].rearrange("q (w f) -> q w f", f=ROW_VALUES)[:, first + 1 : first + 1 + rows]
-            grid = images[n][:].rearrange("q (v e l) -> q v e l", v=2, e=PAIR)[:, 0, :, 0 : rows * H]
+            grid = images[n][:].rearrange("q (v e l) -> q v e l", v=2, e=LANES)[:, 0, :, local * H : (local + rows) * H]
             grid = grid.rearrange("q e (i r) -> q i e r", r=H)
             engine_copy(out=values[:, :, 1:4:2], in_=grid[:, :, :, 0])
             engine_copy(out=values[:, :, ROW_VALUES - 4 : ROW_VALUES - 1 : 2], in_=grid[:, :, :, H - 1])
 
-        def quantise(n, start, end, di):
-            b = pieces[n][0]
+        def quantise(unit, di):
+            b, start, end = unit
             nc.vector.quantize_mx(
                 out=p_codes[b, di][:, start * H_OUT : end * H_OUT].bitcast(FP8X4),
                 scales=p_scales[b, di][:, start * H_OUT : end * H_OUT],
@@ -120,73 +123,105 @@ def tile_conv2d_s_kernel(tc, x, K, out):
         results = []
         for b in range(BATCH):
             results.append(keep.tile([P, H_OUT * H_OUT], F32, name="result_%d" % b))
+        accs = {}
 
-        pending = []
-
-        def products(n):
-            b = pieces[n][0]
-            for start, end in units[n]:
-                acc = banks.tile([P, (end - start) * H_OUT], F32, name="acc_%d_%d" % (b, start))
-                some = slice(start * H_OUT, end * H_OUT)
-                for di in range(DI):
-                    nc.tensor.matmul_mx(
-                        out=acc[:],
-                        lhsT=k_codes[:, di].bitcast(FP8X4),
-                        lhsT_scale=k_scales[:, di],
-                        rhs=p_codes[b, di][:, some].bitcast(FP8X4),
-                        rhs_scale=p_scales[b, di][:, some],
-                        start=(di == 0),
-                        stop=(di == DI - 1),
-                    )
-                pending.append((b, start, end, acc))
-
-        def leave(b, start, end, acc):
-                some = slice(start * H_OUT, end * H_OUT)
-                nc.scalar.copy(
-                    out=results[b][:, some].rearrange("o (i m jp) -> o i m jp", m=HALF, jp=2),
-                    in_=acc[:].rearrange("o (i jp m) -> o i m jp", jp=2, m=HALF),
-                )
-                nc.sync.dma_start(out=out[b].rearrange("o i j -> o (i j)")[:, some], in_=results[b][:, some])
-
-        def group_k():
+        def multiply(unit):
+            b, start, end = unit
+            acc = banks.tile([P, (end - start) * H_OUT], F32, name="acc_%d_%d" % (b, start))
+            accs[unit] = acc
+            some = slice(start * H_OUT, end * H_OUT)
             for di in range(DI):
-                nc.vector.tensor_copy(
-                    out=k_grouped[:, di],
-                    in_=k_rows[:, :, di * DJ * C_OUT : (di + 1) * DJ * C_OUT].rearrange("q e (t o) -> q o e t", t=DJ),
+                nc.tensor.matmul_mx(
+                    out=acc[:],
+                    lhsT=k_codes[:, di].bitcast(FP8X4),
+                    lhsT_scale=k_scales[:, di],
+                    rhs=p_codes[b, di][:, some].bitcast(FP8X4),
+                    rhs_scale=p_scales[b, di][:, some],
+                    start=(di == 0),
+                    stop=(di == DI - 1),
                 )
+
+        def leave(engine_copy, unit):
+            b, start, end = unit
+            some = slice(start * H_OUT, end * H_OUT)
+            engine_copy(
+                out=results[b][:, some].rearrange("o (i m jp) -> o i m jp", m=HALF, jp=2),
+                in_=accs[unit][:].rearrange("o (i jp m) -> o i m jp", jp=2, m=HALF),
+            )
+            nc.sync.dma_start(out=out[b].rearrange("o i j -> o (i j)")[:, some], in_=results[b][:, some])
+
+        def group_k(di):
+            nc.vector.tensor_copy(
+                out=k_grouped[:, di],
+                in_=k_rows[:, :, di * DJ * C_OUT : (di + 1) * DJ * C_OUT].rearrange("q e (t o) -> q o e t", t=DJ),
+            )
+
+        def quantise_k():
             nc.vector.quantize_mx(
                 out=k_codes[:].rearrange("q g o -> q (g o)").bitcast(FP8X4),
                 scales=k_scales[:].rearrange("q g o -> q (g o)"),
                 in_=k_grouped[:].rearrange("q g o e t -> q (g o e t)"),
             )
 
-        group_k()
+        def scalar_windows(g, even_copy=True, odd_copy=True):
+            if even_copy:
+                build_class(nc.scalar.copy, g, 0, 1)
+                build_class(nc.scalar.copy, g, 1, 0)
+                build_edges(nc.scalar.copy, g)
+            if odd_copy:
+                build_class(nc.scalar.copy, g, 0, 0)
+                build_class(nc.scalar.copy, g, 1, 1)
 
-        def build_scalar(n):
+        def vector_part(n):
+            make_odd(n)
+            build_class(nc.vector.tensor_copy, n, 1, 1)
+
+        def scalar_even(n):
             build_class(nc.scalar.copy, n, 0, 1)
             build_class(nc.scalar.copy, n, 1, 0)
             build_edges(nc.scalar.copy, n)
+
+        def scalar_odd(n):
             build_class(nc.scalar.copy, n, 0, 0)
 
-        def build_vector(n):
-            build_class(nc.vector.tensor_copy, n, 1, 1)
-
-        build_vector(0)
-        build_scalar(0)
+        u = units
+        load_image(0)
+        load_k()
+        warm_up()
+        for b in range(BATCH):
+            clear(b)
+        load_image(1)
+        vector_part(0)
+        scalar_even(0)
         load_image(2)
-        build_scalar(1)
+        scalar_odd(0)
+        group_k(0)
+        group_k(1)
+        scalar_even(1)
         load_image(3)
-        for n in range(len(pieces)):
-            first_calls = True
-            for start, end in units[n]:
-                quantise(n, start, end, 0)
-                if first_calls and n + 1 < len(pieces):
-                    build_vector(n + 1)
-                first_calls = False
-                quantise(n, start, end, 1)
-            if n + 2 < len(pieces):
-                build_scalar(n + 2)
-            products(n)
-            for item in pending:
-                leave(*item)
-            pending.clear()
+        quantise(u[0], 0)
+        vector_part(1)
+        scalar_odd(1)
+        quantise(u[0], 1)
+        quantise_k()
+        scalar_even(2)
+        multiply(u[0])
+        quantise(u[1], 0)
+        vector_part(2)
+        scalar_odd(2)
+        quantise(u[1], 1)
+        multiply(u[1])
+        leave(nc.scalar.copy, u[0])
+        scalar_even(3)
+        quantise(u[2], 0)
+        vector_part(3)
+        scalar_odd(3)
+        quantise(u[2], 1)
+        multiply(u[2])
+        leave(nc.scalar.copy, u[1])
+        for unit in u[3:]:
+            quantise(unit, 0)
+            quantise(unit, 1)
+            multiply(unit)
+        for unit in u[2:]:
+            leave(nc.scalar.copy, unit)

@@ -55,32 +55,36 @@ def tile_conv2d_s_kernel(tc, x, K, out):
                 p_codes[b, di] = keep.tile([P, H_OUT * H_OUT], U32, name="codes_%d_%d" % (b, di), align_bytes=64)
                 p_scales[b, di] = keep.tile([P, H_OUT * H_OUT], U8, name="scales_%d_%d" % (b, di), align_bytes=64)
 
-        def load_lanes(to, channels):
-            nc.sync.dma_start(out=to[:, 0], in_=channels[HALFP : HALFP + P])
-            nc.sync.dma_start(out=to[0:HALFP, 1], in_=channels[0:HALFP])
-            nc.scalar.dma_start(out=to[HALFP:P, 1], in_=channels[P + HALFP : 2 * P])
+        def load_lane_0(to, channels):
+            nc.sync.dma_start(out=to, in_=channels[HALFP : HALFP + P])
+
+        def load_lane_1(to, channels):
+            nc.sync.dma_start(out=to[0:HALFP], in_=channels[0:HALFP])
+            nc.scalar.dma_start(out=to[HALFP:P], in_=channels[P + HALFP : 2 * P])
 
         def load_k():
-            load_lanes(k_rows, K.rearrange("kh kw c o -> (kh kw c) o").rearrange("(c t) o -> c (t o)", t=DI * DJ))
+            rows = K.rearrange("kh kw c o -> (kh kw c) o").rearrange("(c t) o -> c (t o)", t=DI * DJ)
+            load_lane_0(k_rows[:, 0], rows)
+            load_lane_1(k_rows[:, 1], rows)
 
-        def load_image(n):
+        def load_copy(n, v, lanes):
             b, first, rows = pieces[n]
-            lanes = images[n][:].rearrange("q (v e l) -> q v e l", v=2, e=LANES)
-            channels = x[b].rearrange("c i j -> c (i j)")[:, first * H : (first + rows) * H]
-            load_lanes(lanes[:, 0, :, 0 : rows * H], channels)
-            nc.sync.dma_start(out=lanes[:, 1, 0, 0 : rows * H - 1], in_=channels[HALFP : HALFP + P, 1:])
+            to = images[n][:].rearrange("q (v e l) -> q v e l", v=2, e=LANES)[:, v, :, 0 : rows * H - v]
+            channels = x[b].rearrange("c i j -> c (i j)")[:, first * H + v : (first + rows) * H]
+            for e in lanes:
+                [load_lane_0, load_lane_1][e](to[:, e], channels)
 
-        def make_odd(n):
+        def make_odd(n, first_lane):
             rows = pieces[n][2]
-            lanes = images[n][:].rearrange("q (v e l) -> q v e l", v=2, e=LANES)
-            nc.vector.tensor_copy(out=lanes[:, 1, 1, 0 : rows * H - 1], in_=lanes[:, 0, 1, 1 : rows * H])
+            lanes = images[n][:].rearrange("q (v e l) -> q v e l", v=2, e=LANES)[:, :, first_lane:LANES]
+            nc.vector.tensor_copy(out=lanes[:, 1, :, 0 : rows * H - 1], in_=lanes[:, 0, :, 1 : rows * H])
 
         def clear(b):
             words = windows[b][:].bitcast(F32)
             nc.vector.memset(words[:, 0:ROW_WORDS], 0.0)
             nc.vector.memset(words[:, (WINDOW_ROWS - 1) * ROW_WORDS :], 0.0)
-            edges = words[:, ROW_WORDS - 2 : ROW_WORDS - 2 + H_OUT * ROW_WORDS].rearrange("q (w f) -> q w f", f=ROW_WORDS)
-            nc.vector.memset(edges[:, :, 0 : 2 * LANES], 0.0)
+            rows = words.rearrange("q (w f) -> q w f", f=ROW_WORDS)[:, 1 : WINDOW_ROWS - 1]
+            nc.vector.memset(rows[:, :, ROW_WORDS // 2 - LANES : ROW_WORDS // 2 + LANES], 0.0)
 
         def warm_up():
             zeros = keep.tile([P, 1], BF16, name="zeros")
@@ -94,7 +98,7 @@ def tile_conv2d_s_kernel(tc, x, K, out):
             local = first - pieces[n][1]
             count = (rows - ip + 1) // 2
             words = windows[b][:].bitcast(F32).rearrange("q (w f) -> q w f", f=ROW_WORDS)
-            start = H_OUT if odd else LANES
+            start = 0 if odd else (HALF + 1) * LANES
             to = words[:, first + 1 + ip : first + 1 + rows : 2, start : start + INNER * LANES]
             copy = (ip + 1 - odd) % 2
             lanes = images[n][:].bitcast(F32).rearrange("q (v e l) -> q v e l", v=2, e=LANES)
@@ -109,8 +113,9 @@ def tile_conv2d_s_kernel(tc, x, K, out):
             values = windows[b][:].rearrange("q (w f) -> q w f", f=ROW_VALUES)[:, first + 1 : first + 1 + rows]
             grid = images[n][:].rearrange("q (v e l) -> q v e l", v=2, e=LANES)[:, 0, :, local * H : (local + rows) * H]
             grid = grid.rearrange("q e (i r) -> q i e r", r=H)
-            engine_copy(out=values[:, :, 1:4:2], in_=grid[:, :, :, 0])
-            engine_copy(out=values[:, :, ROW_VALUES - 4 : ROW_VALUES - 1 : 2], in_=grid[:, :, :, H - 1])
+            both = values[:, :, ROW_VALUES // 2 - PACK : ROW_VALUES // 2 - PACK + 10].rearrange("q w (s v) -> q w s v", s=2)
+            ends = grid[:, :, :, 0 : H : H - 1][:, :, :, ::-1]
+            engine_copy(out=both[:, :, :, 0:3:2], in_=ends.rearrange("q i e s -> q i s e"))
 
         def quantise(unit, di):
             b, start, end = unit
@@ -146,7 +151,7 @@ def tile_conv2d_s_kernel(tc, x, K, out):
             some = slice(start * H_OUT, end * H_OUT)
             engine_copy(
                 out=results[b][:, some].rearrange("o (i m jp) -> o i m jp", m=HALF, jp=2),
-                in_=accs[unit][:].rearrange("o (i jp m) -> o i m jp", jp=2, m=HALF),
+                in_=accs[unit][:].rearrange("o (i jp m) -> o i m jp", jp=2, m=HALF)[:, :, :, ::-1],
             )
             nc.sync.dma_start(out=out[b].rearrange("o i j -> o (i j)")[:, some], in_=results[b][:, some])
 
@@ -163,65 +168,64 @@ def tile_conv2d_s_kernel(tc, x, K, out):
                 in_=k_grouped[:].rearrange("q g o e t -> q (g o e t)"),
             )
 
-        def scalar_windows(g, even_copy=True, odd_copy=True):
-            if even_copy:
-                build_class(nc.scalar.copy, g, 0, 1)
-                build_class(nc.scalar.copy, g, 1, 0)
-                build_edges(nc.scalar.copy, g)
-            if odd_copy:
-                build_class(nc.scalar.copy, g, 0, 0)
-                build_class(nc.scalar.copy, g, 1, 1)
-
-        def vector_part(n):
-            make_odd(n)
-            build_class(nc.vector.tensor_copy, n, 1, 1)
-
-        def scalar_even(n):
-            build_class(nc.scalar.copy, n, 0, 1)
-            build_class(nc.scalar.copy, n, 1, 0)
-            build_edges(nc.scalar.copy, n)
-
-        def scalar_odd(n):
-            build_class(nc.scalar.copy, n, 0, 0)
+        VECTOR = nc.vector.tensor_copy
+        SCALAR = nc.scalar.copy
 
         u = units
-        load_image(0)
+        load_copy(0, 0, [0, 1])
         load_k()
         warm_up()
         for b in range(BATCH):
             clear(b)
-        load_image(1)
-        vector_part(0)
-        scalar_even(0)
-        load_image(2)
-        scalar_odd(0)
+        load_copy(1, 0, [0, 1])
+        load_copy(1, 1, [0])
+        make_odd(0, 0)
+        build_class(VECTOR, 0, 0, 1)
+        build_class(SCALAR, 0, 1, 0)
+        build_edges(SCALAR, 0)
+        load_copy(2, 0, [0, 1])
+        load_copy(2, 1, [0])
+        build_class(SCALAR, 0, 0, 0)
+        build_class(SCALAR, 0, 1, 1)
         group_k(0)
         group_k(1)
-        scalar_even(1)
-        load_image(3)
+        build_class(SCALAR, 1, 1, 0)
+        build_edges(SCALAR, 1)
+        load_copy(3, 0, [0, 1])
+        load_copy(3, 1, [0, 1])
         quantise(u[0], 0)
-        vector_part(1)
-        scalar_odd(1)
+        make_odd(1, 1)
+        build_class(VECTOR, 1, 0, 1)
+        build_class(SCALAR, 1, 0, 0)
+        build_class(SCALAR, 1, 1, 1)
         quantise(u[0], 1)
         quantise_k()
-        scalar_even(2)
         multiply(u[0])
+        build_class(SCALAR, 2, 0, 1)
+        build_class(SCALAR, 2, 1, 0)
+        build_edges(SCALAR, 2)
+        make_odd(2, 1)
+        build_class(SCALAR, 2, 0, 0)
+        build_class(SCALAR, 2, 1, 1)
         quantise(u[1], 0)
-        vector_part(2)
-        scalar_odd(2)
         quantise(u[1], 1)
         multiply(u[1])
-        leave(nc.scalar.copy, u[0])
-        scalar_even(3)
+        build_class(SCALAR, 3, 0, 1)
+        build_class(SCALAR, 3, 1, 0)
+        build_edges(SCALAR, 3)
+        build_class(SCALAR, 3, 0, 0)
+        build_class(SCALAR, 3, 1, 1)
         quantise(u[2], 0)
-        vector_part(3)
-        scalar_odd(3)
         quantise(u[2], 1)
         multiply(u[2])
-        leave(nc.scalar.copy, u[1])
-        for unit in u[3:]:
-            quantise(unit, 0)
-            quantise(unit, 1)
-            multiply(unit)
-        for unit in u[2:]:
-            leave(nc.scalar.copy, unit)
+        leave(SCALAR, u[0])
+        leave(SCALAR, u[1])
+        quantise(u[3], 0)
+        quantise(u[3], 1)
+        multiply(u[3])
+        quantise(u[4], 0)
+        quantise(u[4], 1)
+        multiply(u[4])
+        leave(SCALAR, u[2])
+        leave(VECTOR, u[3])
+        leave(SCALAR, u[4])

@@ -30,7 +30,7 @@ FLOPS = 2 * BATCH * H_OUT * H_OUT * 256 * PACK * C_OUT
 def tile_conv2d_s_kernel(tc, x, K, out):
     nc = tc.nc
     pieces = [(0, 0, 16), (0, 16, 15), (1, 0, 16), (1, 16, 15)]
-    groups = [(0, 0, 16), (1, 16, 15), (2, 0, 16), (3, 16, 15)]
+    odd_pieces = [(0, 0, 16), (0, 16, 15), (1, 0, 31)]
     units = [(0, 0, 16), (0, 16, 32), (1, 0, 16), (1, 16, 24), (1, 24, 32)]
     with ExitStack() as ctx:
         keep = ctx.enter_context(tc.tile_pool(name="keep", bufs=1))
@@ -42,10 +42,23 @@ def tile_conv2d_s_kernel(tc, x, K, out):
         k_codes = keep.tile([P, DI, C_OUT], U32, name="k_codes", align_bytes=64)
         k_scales = keep.tile([P, DI, C_OUT], U8, name="k_scales", align_bytes=64)
 
-        lengths = [-(-(H * rows + 64) // 16) * 16 for b, first, rows in pieces]
-        images = []
-        for n in range(len(pieces)):
-            images.append(keep.tile([P, 2 * LANES * lengths[n]], BF16, name="image_%d" % n))
+        def lanes_tile(rows, name):
+            length = -(-(H * rows + 64) // 16) * 16
+            return keep.tile([P, LANES * length], BF16, name=name)
+
+        evens = {}
+        for piece in pieces:
+            evens[piece] = lanes_tile(piece[2], "even_%d_%d" % piece[:2])
+        odds = {}
+        for piece in odd_pieces:
+            odds[piece] = lanes_tile(piece[2], "odd_%d_%d" % piece[:2])
+
+        def odd_piece_of(piece):
+            return [o for o in odd_pieces if o[0] == piece[0] and o[1] <= piece[1] < o[1] + o[2]][0]
+
+        def lanes_of(tile):
+            return tile[:].rearrange("q (e l) -> q e l", e=LANES)
+
         windows = []
         p_codes = {}
         p_scales = {}
@@ -58,26 +71,39 @@ def tile_conv2d_s_kernel(tc, x, K, out):
         def load_lane_0(to, channels):
             nc.sync.dma_start(out=to, in_=channels[HALFP : HALFP + P])
 
-        def load_lane_1(to, channels):
+        def load_lane_1(to, channels, second_half=nc.scalar):
             nc.sync.dma_start(out=to[0:HALFP], in_=channels[0:HALFP])
-            nc.scalar.dma_start(out=to[HALFP:P], in_=channels[P + HALFP : 2 * P])
+            second_half.dma_start(out=to[HALFP:P], in_=channels[P + HALFP : 2 * P])
 
         def load_k():
             rows = K.rearrange("kh kw c o -> (kh kw c) o").rearrange("(c t) o -> c (t o)", t=DI * DJ)
             load_lane_0(k_rows[:, 0], rows)
             load_lane_1(k_rows[:, 1], rows)
 
-        def load_copy(n, v, lanes):
-            b, first, rows = pieces[n]
-            to = images[n][:].rearrange("q (v e l) -> q v e l", v=2, e=LANES)[:, v, :, 0 : rows * H - v]
+        def load_rows(to, part, v, lanes, second_half=nc.scalar):
+            b, first, rows = part
             channels = x[b].rearrange("c i j -> c (i j)")[:, first * H + v : (first + rows) * H]
-            for e in lanes:
-                [load_lane_0, load_lane_1][e](to[:, e], channels)
+            if 0 in lanes:
+                load_lane_0(to[:, 0, 0 : rows * H - v], channels)
+            if 1 in lanes:
+                load_lane_1(to[:, 1, 0 : rows * H - v], channels, second_half)
+
+        def load_even(n, lanes, second_half=nc.scalar):
+            load_rows(lanes_of(evens[pieces[n]]), pieces[n], 0, lanes, second_half)
+
+        def load_odd(m, lanes, second_half=nc.scalar):
+            load_rows(lanes_of(odds[odd_pieces[m]]), odd_pieces[m], 1, lanes, second_half)
+
+        def load_odd_part(m, n, lanes, second_half=nc.scalar):
+            start = (pieces[n][1] - odd_pieces[m][1]) * H
+            load_rows(lanes_of(odds[odd_pieces[m]])[:, :, start:], pieces[n], 1, lanes, second_half)
 
         def make_odd(n, first_lane):
-            rows = pieces[n][2]
-            lanes = images[n][:].rearrange("q (v e l) -> q v e l", v=2, e=LANES)[:, :, first_lane:LANES]
-            nc.vector.tensor_copy(out=lanes[:, 1, :, 0 : rows * H - 1], in_=lanes[:, 0, :, 1 : rows * H])
+            size = pieces[n][2] * H
+            nc.vector.tensor_copy(
+                out=lanes_of(odds[odd_piece_of(pieces[n])])[:, first_lane:, 0 : size - 1],
+                in_=lanes_of(evens[pieces[n]])[:, first_lane:, 1:size],
+            )
 
         def clear(b):
             words = windows[b][:].bitcast(F32)
@@ -92,27 +118,27 @@ def tile_conv2d_s_kernel(tc, x, K, out):
             nc.vector.memset(zeros[:], 0.0)
             nc.scalar.copy(out=warm[:], in_=zeros[:])
 
-        def build_class(engine_copy, g, ip, odd):
-            n, first, rows = groups[g]
-            b = pieces[n][0]
-            local = first - pieces[n][1]
+        def build_class(engine_copy, n, ip, odd):
+            piece = pieces[n]
+            b, first, rows = piece
             count = (rows - ip + 1) // 2
             words = windows[b][:].bitcast(F32).rearrange("q (w f) -> q w f", f=ROW_WORDS)
             start = 0 if odd else (HALF + 1) * LANES
             to = words[:, first + 1 + ip : first + 1 + rows : 2, start : start + INNER * LANES]
-            copy = (ip + 1 - odd) % 2
-            lanes = images[n][:].bitcast(F32).rearrange("q (v e l) -> q v e l", v=2, e=LANES)
-            at = local * H // 2 + [0, 15 if odd else 16][ip]
-            grid = lanes[:, copy, :, at : at + count * H].rearrange("q e (a r) -> q e a r", r=H)[:, :, :, 0:INNER]
+            at = [0, 15 if odd else 16][ip]
+            tile = evens[piece]
+            if ip == odd:
+                part = odd_piece_of(piece)
+                tile = odds[part]
+                at += (first - part[1]) * H // 2
+            grid = tile[:].bitcast(F32).rearrange("q (e l) -> q e l", e=LANES)[:, :, at : at + count * H]
+            grid = grid.rearrange("q e (a r) -> q e a r", r=H)[:, :, :, 0:INNER]
             engine_copy(out=to.rearrange("q a (k e) -> q a k e", e=LANES), in_=grid.rearrange("q e a k -> q a k e"))
 
-        def build_edges(engine_copy, g):
-            n, first, rows = groups[g]
-            b = pieces[n][0]
-            local = first - pieces[n][1]
+        def build_edges(engine_copy, n):
+            b, first, rows = pieces[n]
             values = windows[b][:].rearrange("q (w f) -> q w f", f=ROW_VALUES)[:, first + 1 : first + 1 + rows]
-            grid = images[n][:].rearrange("q (v e l) -> q v e l", v=2, e=LANES)[:, 0, :, local * H : (local + rows) * H]
-            grid = grid.rearrange("q e (i r) -> q i e r", r=H)
+            grid = lanes_of(evens[pieces[n]])[:, :, 0 : rows * H].rearrange("q e (i r) -> q i e r", r=H)
             both = values[:, :, ROW_VALUES // 2 - PACK : ROW_VALUES // 2 - PACK + 10].rearrange("q w (s v) -> q w s v", s=2)
             ends = grid[:, :, :, 0 : H : H - 1][:, :, :, ::-1]
             engine_copy(out=both[:, :, :, 0:3:2], in_=ends.rearrange("q i e s -> q i s e"))
@@ -155,8 +181,8 @@ def tile_conv2d_s_kernel(tc, x, K, out):
             )
             nc.sync.dma_start(out=out[b].rearrange("o i j -> o (i j)")[:, some], in_=results[b][:, some])
 
-        def group_k(di):
-            nc.vector.tensor_copy(
+        def group_k(di, engine_copy=nc.vector.tensor_copy):
+            engine_copy(
                 out=k_grouped[:, di],
                 in_=k_rows[:, :, di * DJ * C_OUT : (di + 1) * DJ * C_OUT].rearrange("q e (t o) -> q o e t", t=DJ),
             )
@@ -172,30 +198,30 @@ def tile_conv2d_s_kernel(tc, x, K, out):
         SCALAR = nc.scalar.copy
 
         u = units
-        load_copy(0, 0, [0, 1])
+        load_even(0, [0, 1])
         load_k()
         warm_up()
         for b in range(BATCH):
             clear(b)
-        load_copy(1, 0, [0, 1])
-        load_copy(1, 1, [0])
+        load_even(1, [0, 1], nc.gpsimd)
         make_odd(0, 0)
         build_class(VECTOR, 0, 0, 1)
         build_class(SCALAR, 0, 1, 0)
         build_edges(SCALAR, 0)
-        load_copy(2, 0, [0, 1])
-        load_copy(2, 1, [0])
+        load_even(2, [0, 1], nc.sync)
+        load_odd(2, [0])
+        load_odd_part(2, 2, [1], nc.sync)
         build_class(SCALAR, 0, 0, 0)
         build_class(SCALAR, 0, 1, 1)
         group_k(0)
         group_k(1)
+        make_odd(1, 0)
+        build_class(SCALAR, 1, 0, 1)
         build_class(SCALAR, 1, 1, 0)
         build_edges(SCALAR, 1)
-        load_copy(3, 0, [0, 1])
-        load_copy(3, 1, [0, 1])
+        load_even(3, [0, 1], nc.sync)
+        load_odd_part(2, 3, [1], nc.sync)
         quantise(u[0], 0)
-        make_odd(1, 1)
-        build_class(VECTOR, 1, 0, 1)
         build_class(SCALAR, 1, 0, 0)
         build_class(SCALAR, 1, 1, 1)
         quantise(u[0], 1)
@@ -204,7 +230,6 @@ def tile_conv2d_s_kernel(tc, x, K, out):
         build_class(SCALAR, 2, 0, 1)
         build_class(SCALAR, 2, 1, 0)
         build_edges(SCALAR, 2)
-        make_odd(2, 1)
         build_class(SCALAR, 2, 0, 0)
         build_class(SCALAR, 2, 1, 1)
         quantise(u[1], 0)

@@ -156,29 +156,35 @@ def tile_conv2d_s_kernel(tc, x, K, out):
             results.append(keep.tile([P, H_OUT * H_OUT], F32, name="result_%d" % b))
         accs = {}
 
-        def multiply(unit):
+        def multiply(unit, parts=1):
             b, start, end = unit
-            acc = banks.tile([P, (end - start) * H_OUT], F32, name="acc_%d_%d" % (b, start))
-            accs[unit] = acc
-            some = slice(start * H_OUT, end * H_OUT)
+            rows = (end - start) // parts
+            accs[unit] = []
+            for first in range(start, end, rows):
+                accs[unit].append(banks.tile([P, rows * H_OUT], F32, name="acc_%d_%d" % (b, first)))
             for di in range(DI):
-                nc.tensor.matmul_mx(
-                    out=acc[:],
-                    lhsT=k_codes[:, di].bitcast(FP8X4),
-                    lhsT_scale=k_scales[:, di],
-                    rhs=p_codes[b, di][:, some].bitcast(FP8X4),
-                    rhs_scale=p_scales[b, di][:, some],
-                    start=(di == 0),
-                    stop=(di == DI - 1),
-                )
+                for n in range(parts):
+                    some = slice((start + n * rows) * H_OUT, (start + (n + 1) * rows) * H_OUT)
+                    nc.tensor.matmul_mx(
+                        out=accs[unit][n][:],
+                        lhsT=k_codes[:, di].bitcast(FP8X4),
+                        lhsT_scale=k_scales[:, di],
+                        rhs=p_codes[b, di][:, some].bitcast(FP8X4),
+                        rhs_scale=p_scales[b, di][:, some],
+                        start=(di == 0),
+                        stop=(di == DI - 1),
+                    )
 
-        def leave(engine_copy, unit):
+        def leave(engine_copies, unit):
             b, start, end = unit
+            rows = (end - start) // len(engine_copies)
+            for n in range(len(engine_copies)):
+                some = slice((start + n * rows) * H_OUT, (start + (n + 1) * rows) * H_OUT)
+                engine_copies[n](
+                    out=results[b][:, some].rearrange("o (i m jp) -> o i m jp", m=HALF, jp=2),
+                    in_=accs[unit][n][:].rearrange("o (i jp m) -> o i m jp", jp=2, m=HALF)[:, :, :, ::-1],
+                )
             some = slice(start * H_OUT, end * H_OUT)
-            engine_copy(
-                out=results[b][:, some].rearrange("o (i m jp) -> o i m jp", m=HALF, jp=2),
-                in_=accs[unit][:].rearrange("o (i jp m) -> o i m jp", jp=2, m=HALF)[:, :, :, ::-1],
-            )
             nc.sync.dma_start(out=out[b].rearrange("o i j -> o (i j)")[:, some], in_=results[b][:, some])
 
         def group_k(di, engine_copy=nc.vector.tensor_copy):
@@ -235,22 +241,22 @@ def tile_conv2d_s_kernel(tc, x, K, out):
         quantise(u[1], 0)
         quantise(u[1], 1)
         multiply(u[1])
-        build_class(SCALAR, 3, 0, 1)
         build_class(SCALAR, 3, 1, 0)
         build_edges(SCALAR, 3)
         build_class(SCALAR, 3, 0, 0)
         build_class(SCALAR, 3, 1, 1)
+        build_class(VECTOR, 3, 0, 1)
         quantise(u[2], 0)
         quantise(u[2], 1)
-        multiply(u[2])
-        leave(SCALAR, u[0])
-        leave(SCALAR, u[1])
+        multiply(u[2], 2)
+        leave([SCALAR], u[0])
+        leave([SCALAR], u[1])
         quantise(u[3], 0)
         quantise(u[3], 1)
         multiply(u[3])
         quantise(u[4], 0)
         quantise(u[4], 1)
-        multiply(u[4])
-        leave(SCALAR, u[2])
-        leave(VECTOR, u[3])
-        leave(SCALAR, u[4])
+        multiply(u[4], 2)
+        leave([SCALAR, SCALAR], u[2])
+        leave([SCALAR], u[3])
+        leave([VECTOR, SCALAR], u[4])

from contextlib import ExitStack

import concourse.mybir as mybir

BF16 = mybir.dt.bfloat16
F32 = mybir.dt.float32
U32 = mybir.dt.uint32
U8 = mybir.dt.uint8
FP8X4 = mybir.dt.float8_e4m3fn_x4

P = 128
PACK = 4
BATCH = 2
C_OUT = 128
H = 31
H_OUT = 32
HALFP = P // 2
LANES = 2
DI = 2
DJ = 2
HALF = H_OUT // 2
ROW_WORDS = H_OUT * LANES
ROW_VALUES = ROW_WORDS * DJ
WINDOW_ROWS = H_OUT + 1
INNER = HALF - 1

FLOPS = 2 * BATCH * H_OUT * H_OUT * 256 * PACK * C_OUT


def tile_conv2d_s_kernel(tc, x, K, out):
    nc = tc.nc
    pieces = [(0, 0, 16), (0, 16, 15), (1, 0, 16), (1, 16, 15)]
    odd_pieces = [(0, 0, 16), (0, 16, 15), (1, 0, 31)]
    units = [(0, 0, 16), (0, 16, 32), (1, 0, 16), (1, 16, 24), (1, 24, 32)]
    with ExitStack() as ctx:
        keep = ctx.enter_context(tc.tile_pool(name="keep", bufs=1))
        banks = ctx.enter_context(tc.psum_pool(name="banks", bufs=1))
        ctx.enter_context(tc.manual_schedule())

        k_rows = keep.tile([P, LANES, DI * DJ * C_OUT], BF16, name="k_rows")
        k_grouped = keep.tile([P, DI, C_OUT, LANES, DJ], BF16, name="k_grouped", align_bytes=64)
        k_codes = keep.tile([P, DI, C_OUT], U32, name="k_codes", align_bytes=64)
        k_scales = keep.tile([P, DI, C_OUT], U8, name="k_scales", align_bytes=64)

        def lanes_tile(rows, name):
            length = -(-(H * rows + 64) // 16) * 16
            return keep.tile([P, LANES * length], BF16, name=name)

        evens = {}
        for piece in pieces:
            evens[piece] = lanes_tile(piece[2], "even_%d_%d" % piece[:2])
        odds = {}
        for piece in odd_pieces:
            odds[piece] = lanes_tile(piece[2], "odd_%d_%d" % piece[:2])

        def odd_piece_of(piece):
            return [o for o in odd_pieces if o[0] == piece[0] and o[1] <= piece[1] < o[1] + o[2]][0]

        def lanes_of(tile):
            return tile[:].rearrange("q (e l) -> q e l", e=LANES)

        windows = []
        p_codes = {}
        p_scales = {}
        for b in range(BATCH):
            windows.append(keep.tile([P, WINDOW_ROWS * ROW_VALUES], BF16, name="windows_%d" % b, align_bytes=64))
            for di in range(DI):
                p_codes[b, di] = keep.tile([P, H_OUT * H_OUT], U32, name="codes_%d_%d" % (b, di), align_bytes=64)
                p_scales[b, di] = keep.tile([P, H_OUT * H_OUT], U8, name="scales_%d_%d" % (b, di), align_bytes=64)

        def load_lane_0(to, channels):
            nc.sync.dma_start(out=to, in_=channels[HALFP : HALFP + P])

        def load_lane_1(to, channels, second_half=nc.scalar):
            nc.sync.dma_start(out=to[0:HALFP], in_=channels[0:HALFP])
            second_half.dma_start(out=to[HALFP:P], in_=channels[P + HALFP : 2 * P])

        def load_k():
            rows = K.rearrange("kh kw c o -> (kh kw c) o").rearrange("(c t) o -> c (t o)", t=DI * DJ)
            load_lane_0(k_rows[:, 0], rows)
            load_lane_1(k_rows[:, 1], rows)

        def load_rows(to, part, v, lanes, second_half=nc.scalar):
            b, first, rows = part
            channels = x[b].rearrange("c i j -> c (i j)")[:, first * H + v : (first + rows) * H]
            if 0 in lanes:
                load_lane_0(to[:, 0, 0 : rows * H - v], channels)
            if 1 in lanes:
                load_lane_1(to[:, 1, 0 : rows * H - v], channels, second_half)

        def load_even(n, lanes, second_half=nc.scalar):
            load_rows(lanes_of(evens[pieces[n]]), pieces[n], 0, lanes, second_half)

        def load_odd(m, lanes, second_half=nc.scalar):
            load_rows(lanes_of(odds[odd_pieces[m]]), odd_pieces[m], 1, lanes, second_half)

        def load_odd_part(m, n, lanes, second_half=nc.scalar):
            start = (pieces[n][1] - odd_pieces[m][1]) * H
            load_rows(lanes_of(odds[odd_pieces[m]])[:, :, start:], pieces[n], 1, lanes, second_half)

        def make_odd(n, first_lane):
            size = pieces[n][2] * H
            nc.vector.tensor_copy(
                out=lanes_of(odds[odd_piece_of(pieces[n])])[:, first_lane:, 0 : size - 1],
                in_=lanes_of(evens[pieces[n]])[:, first_lane:, 1:size],
            )

        def clear(b):
            words = windows[b][:].bitcast(F32)
            nc.vector.memset(words[:, 0:ROW_WORDS], 0.0)
            nc.vector.memset(words[:, (WINDOW_ROWS - 1) * ROW_WORDS :], 0.0)
            rows = words.rearrange("q (w f) -> q w f", f=ROW_WORDS)[:, 1 : WINDOW_ROWS - 1]
            nc.vector.memset(rows[:, :, ROW_WORDS // 2 - LANES : ROW_WORDS // 2 + LANES], 0.0)

        def warm_up():
            zeros = keep.tile([P, 1], BF16, name="zeros")
            warm = keep.tile([P, 1], BF16, name="warm")
            nc.vector.memset(zeros[:], 0.0)
            nc.scalar.copy(out=warm[:], in_=zeros[:])

        def build_class(engine_copy, n, ip, odd):
            piece = pieces[n]
            b, first, rows = piece
            count = (rows - ip + 1) // 2
            words = windows[b][:].bitcast(F32).rearrange("q (w f) -> q w f", f=ROW_WORDS)
            start = 0 if odd else (HALF + 1) * LANES
            to = words[:, first + 1 + ip : first + 1 + rows : 2, start : start + INNER * LANES]
            at = [0, 15 if odd else 16][ip]
            tile = evens[piece]
            if ip == odd:
                part = odd_piece_of(piece)
                tile = odds[part]
                at += (first - part[1]) * H // 2
            grid = tile[:].bitcast(F32).rearrange("q (e l) -> q e l", e=LANES)[:, :, at : at + count * H]
            grid = grid.rearrange("q e (a r) -> q e a r", r=H)[:, :, :, 0:INNER]
            engine_copy(out=to.rearrange("q a (k e) -> q a k e", e=LANES), in_=grid.rearrange("q e a k -> q a k e"))

        def build_edges(engine_copy, n):
            b, first, rows = pieces[n]
            values = windows[b][:].rearrange("q (w f) -> q w f", f=ROW_VALUES)[:, first + 1 : first + 1 + rows]
            grid = lanes_of(evens[pieces[n]])[:, :, 0 : rows * H].rearrange("q e (i r) -> q i e r", r=H)
            both = values[:, :, ROW_VALUES // 2 - PACK : ROW_VALUES // 2 - PACK + 10].rearrange("q w (s v) -> q w s v", s=2)
            ends = grid[:, :, :, 0 : H : H - 1][:, :, :, ::-1]
            engine_copy(out=both[:, :, :, 0:3:2], in_=ends.rearrange("q i e s -> q i s e"))

        def quantise(unit, di):
            b, start, end = unit
            nc.vector.quantize_mx(
                out=p_codes[b, di][:, start * H_OUT : end * H_OUT].bitcast(FP8X4),
                scales=p_scales[b, di][:, start * H_OUT : end * H_OUT],
                in_=windows[b][:, (start + di) * ROW_VALUES : (end + di) * ROW_VALUES],
            )

        results = []
        for b in range(BATCH):
            results.append(keep.tile([P, H_OUT * H_OUT], F32, name="result_%d" % b))
        accs = {}

        def multiply(unit, parts=1):
            b, start, end = unit
            rows = (end - start) // parts
            accs[unit] = []
            for first in range(start, end, rows):
                accs[unit].append(banks.tile([P, rows * H_OUT], F32, name="acc_%d_%d" % (b, first)))
            for di in range(DI):
                for n in range(parts):
                    some = slice((start + n * rows) * H_OUT, (start + (n + 1) * rows) * H_OUT)
                    nc.tensor.matmul_mx(
                        out=accs[unit][n][:],
                        lhsT=k_codes[:, di].bitcast(FP8X4),
                        lhsT_scale=k_scales[:, di],
                        rhs=p_codes[b, di][:, some].bitcast(FP8X4),
                        rhs_scale=p_scales[b, di][:, some],
                        start=(di == 0),
                        stop=(di == DI - 1),
                    )

        def leave(engine_copies, unit):
            b, start, end = unit
            rows = (end - start) // len(engine_copies)
            for n in range(len(engine_copies)):
                some = slice((start + n * rows) * H_OUT, (start + (n + 1) * rows) * H_OUT)
                engine_copies[n](
                    out=results[b][:, some].rearrange("o (i m jp) -> o i m jp", m=HALF, jp=2),
                    in_=accs[unit][n][:].rearrange("o (i jp m) -> o i m jp", jp=2, m=HALF)[:, :, :, ::-1],
                )
            some = slice(start * H_OUT, end * H_OUT)
            nc.sync.dma_start(out=out[b].rearrange("o i j -> o (i j)")[:, some], in_=results[b][:, some])

        def group_k(di, engine_copy=nc.vector.tensor_copy):
            engine_copy(
                out=k_grouped[:, di],
                in_=k_rows[:, :, di * DJ * C_OUT : (di + 1) * DJ * C_OUT].rearrange("q e (t o) -> q o e t", t=DJ),
            )

        def quantise_k():
            nc.vector.quantize_mx(
                out=k_codes[:].rearrange("q g o -> q (g o)").bitcast(FP8X4),
                scales=k_scales[:].rearrange("q g o -> q (g o)"),
                in_=k_grouped[:].rearrange("q g o e t -> q (g o e t)"),
            )

        VECTOR = nc.vector.tensor_copy
        SCALAR = nc.scalar.copy

        u = units
        load_even(0, [0, 1])
        load_k()
        warm_up()
        for b in range(BATCH):
            clear(b)
        load_even(1, [0, 1], nc.gpsimd)
        make_odd(0, 0)
        build_class(VECTOR, 0, 0, 1)
        build_class(SCALAR, 0, 1, 0)
        build_edges(SCALAR, 0)
        load_even(2, [0, 1], nc.sync)
        load_odd(2, [0])
        load_odd_part(2, 2, [1], nc.sync)
        build_class(SCALAR, 0, 0, 0)
        build_class(SCALAR, 0, 1, 1)
        group_k(0)
        group_k(1)
        make_odd(1, 0)
        build_class(SCALAR, 1, 0, 1)
        build_class(SCALAR, 1, 1, 0)
        build_edges(SCALAR, 1)
        load_even(3, [0, 1], nc.sync)
        load_odd_part(2, 3, [1], nc.sync)
        quantise(u[0], 0)
        build_class(SCALAR, 1, 0, 0)
        build_class(SCALAR, 1, 1, 1)
        quantise(u[0], 1)
        quantise_k()
        multiply(u[0])
        build_class(SCALAR, 2, 0, 1)
        build_class(SCALAR, 2, 1, 0)
        build_edges(SCALAR, 2)
        build_class(SCALAR, 2, 0, 0)
        build_class(SCALAR, 2, 1, 1)
        quantise(u[1], 0)
        quantise(u[1], 1)
        multiply(u[1])
        build_class(SCALAR, 3, 1, 0)
        build_edges(SCALAR, 3)
        build_class(SCALAR, 3, 0, 0)
        build_class(SCALAR, 3, 1, 1)
        build_class(VECTOR, 3, 0, 1)
        quantise(u[2], 0)
        quantise(u[2], 1)
        multiply(u[2], 2)
        leave([SCALAR], u[0])
        leave([SCALAR], u[1])
        quantise(u[3], 0)
        quantise(u[3], 1)
        multiply(u[3])
        quantise(u[4], 0)
        quantise(u[4], 1)
        multiply(u[4], 2)
        leave([SCALAR, SCALAR], u[2])
        leave([SCALAR], u[3])
        leave([VECTOR, SCALAR], u[4])
